import numpy as np
import ml_dtypes


def mxq(x, axis, fmt="e4m3"):
    dtype, down = {"e4m3": (ml_dtypes.float8_e4m3fn, 7), "e5m2": (ml_dtypes.float8_e5m2, 14)}[fmt]
    v = np.moveaxis(np.asarray(x, np.float32).astype(ml_dtypes.bfloat16).astype(np.float64), axis, -1)
    blocks = v.reshape(v.shape[:-1] + (-1, 32))
    amax = np.abs(blocks).max(-1, keepdims=True)
    byte = np.maximum(np.where(amax > 0, np.frexp(amax)[1] - 1 + 127, 0) - down, 1)
    scale = np.exp2(byte - 127.0)
    codes = (blocks / scale).astype(np.float32).astype(dtype).astype(np.float64)
    return np.moveaxis((codes * scale).reshape(v.shape), -1, axis)


WIDE = False


def mx_kscale(k):
    if not WIDE:
        return np.ones(k)
    levels = np.array([10, -10, 5, -5, 0])
    if k % 512:
        return np.exp2(np.random.permutation(np.resize(levels, k // 32))).repeat(32)
    a = np.empty((k // 512, 16))
    for p in range(k // 512):
        a[p, :8] = np.random.permutation(np.resize(levels, 8))
        for g in range(8):
            far = levels[np.abs(levels - a[p, g]) >= 10]
            a[p, g + 8] = far[np.random.randint(len(far))]
    return np.exp2(a.ravel()).repeat(32)


BF16 = ml_dtypes.bfloat16


def bf(x):
    return np.asarray(x, np.float32).astype(BF16)


def f64(x):
    return np.asarray(x).astype(np.float64)


E2M1 = np.array([0.0, 0.5, 1.0, 1.5, 2.0, 3.0, 4.0, 6.0, -0.0, -0.5, -1.0, -1.5, -2.0, -3.0, -4.0, -6.0])


def pack_weight(w, fmt):
    k, n = w.shape
    w = f64(bf(w)).reshape(k // 32, 32, n)
    amax = np.abs(w).max(1)
    if fmt == "e4m3":
        byte = np.frexp(amax)[1] - 1 + 127 - 7
    else:
        mant, ex = np.frexp(amax / 6.0)
        byte = np.where(mant > 0.5, ex, ex - 1) + 127
    byte = np.clip(np.where(amax > 0, byte, 1), 1, 254)
    scaled = (w * np.exp2(127.0 - byte)[:, None, :]).reshape(k, n).astype(np.float32)
    by_word = np.ascontiguousarray(scaled.reshape(k // 512, 128, 4, n).transpose(0, 1, 3, 2))
    if fmt == "e4m3":
        words = by_word.astype(ml_dtypes.float8_e4m3fn).view(np.uint8)
    else:
        c = by_word.astype(ml_dtypes.float4_e2m1fn).view(np.uint8) & 0xF
        words = c[..., 0::2] | (c[..., 1::2] << 4)
    return np.ascontiguousarray(words), np.ascontiguousarray(byte.astype(np.uint8).reshape(k // 512, 16, n))


def unpack_weight(words, scales, fmt):
    g, p, n, _ = words.shape
    if fmt == "e4m3":
        vals = np.ascontiguousarray(words).view(ml_dtypes.float8_e4m3fn).astype(np.float64)
    else:
        nib = np.empty((g, p, n, 4), np.uint8)
        nib[..., 0::2] = words & 0xF
        nib[..., 1::2] = words >> 4
        vals = E2M1[nib]
    vals = vals * np.repeat(np.exp2(scales.astype(np.float64) - 127.0), 8, axis=1)[..., None]
    return vals.transpose(0, 1, 3, 2).reshape(g * 512, n)
def pack4(w):
    words, scales = pack_weight(w, "e2m1")
    return words.reshape(words.shape[0], 128, -1), scales


def unpack4(words, scales):
    return unpack_weight(words.reshape(words.shape[0], 128, -1, 2), scales, "e2m1")


B, L, D = 3, 512, 512
SIG = 2.0


def draw0():
    s, t = mx_kscale(D), mx_kscale(D)
    x1 = bf(np.random.standard_normal((B, L, D)) * s)
    words, scales = pack4(np.random.standard_normal((D, D)) * SIG / D / s[:, None] * t)
    return {"x1": x1,
            "bi_linear_w_words": words,
            "bi_linear_w_scales": scales,
            "x2": bf(np.random.standard_normal((B, L, D)) / t)}


def core(x1, bi_linear_w_words, bi_linear_w_scales, x2):
    h = mxq(f64(x1), 2, "e4m3") @ unpack4(bi_linear_w_words, bi_linear_w_scales)
    return mxq(h, 2, "e4m3") @ mxq(f64(x2), 2, "e4m3").transpose(0, 2, 1)


def e4m3fn_bytes(y):
    return np.clip(np.asarray(y, np.float64), -448.0, 448.0).astype(np.float32).astype(ml_dtypes.float8_e4m3fn).view(np.uint8)


def e4m3fn_values(b):
    return np.asarray(b, np.uint8).view(ml_dtypes.float8_e4m3fn).astype(np.float64)


def setup_inputs():
    d = draw0()
    x0 = np.asarray(d['x2']).astype(np.float64)
    s = (np.max(np.abs(x0), axis=(0, 1), keepdims=True) / 448.0).astype(np.float32)
    out = {}
    for k, v in d.items():
        if k == 'x2':
            out['x2_bytes'] = e4m3fn_bytes(x0 / s.astype(np.float64))
            out['x2_scale'] = s
        else:
            out[k] = v
    return out


def reference(x1, bi_linear_w_words, bi_linear_w_scales, x2_bytes, x2_scale):
    return core(x1, bi_linear_w_words, bi_linear_w_scales, e4m3fn_values(x2_bytes) * x2_scale.astype(np.float64))

@@ -1,0 +1,243 @@
+from contextlib import ExitStack
+
+import concourse.mybir as mybir
+from concourse.masks import make_identity
+
+B, L, D = 3, 512, 512
+P = 128
+FLOPS = 2 * 2 * B * L * L * D
+
+F32 = mybir.dt.float32
+BF16 = mybir.dt.bfloat16
+I32 = mybir.dt.int32
+U32 = mybir.dt.uint32
+U8 = mybir.dt.uint8
+E4M3 = mybir.dt.float8_e4m3fn
+FP8X4 = mybir.dt.float8_e4m3fn_x4
+FP4X4 = mybir.dt.float4_e2m1fn_x4
+MULT = mybir.AluOpType.mult
+
+HALVES = 2 * B
+FILL = {0: 2, 1: 1, 2: 2}
+BANKS = {"x1": 1, "x2": 2, "h": 2, "sim": 3}
+ON_VECTOR = (("C2", 3), ("C2", 5), ("HC0", 2), ("HC0", 3), ("HC1", 5), ("OC0", 5), ("OC1", 4),)
+HROWS = 256
+
+
+def tile_coattentionandcombine_pa_w4_kernel(tc, x1, w_words, w_scales, x2_bytes, x2_scale, out):
+    nc = tc.nc
+    with ExitStack() as ctx:
+        keep = ctx.enter_context(tc.tile_pool(name="keep", bufs=1))
+        work = ctx.enter_context(tc.tile_pool(name="work", bufs=6))
+        psum = ctx.enter_context(tc.psum_pool(name="psum", bufs=2))
+        ctx.enter_context(tc.manual_schedule())
+
+        x1_raw = [keep.tile([P, 4 * D], BF16, name="x1_raw%d" % b) for b in range(B)]
+        x2_raw = [keep.tile([P, 4 * D], U8, name="x2_raw%d" % b) for b in range(B)]
+        x2_words = [keep.tile([P, L], U32, name="x2_words%d" % b, align_bytes=64) for b in range(B)]
+        x2_planes = [keep.tile([P, L], U8, name="x2_planes%d" % b, align_bytes=64) for b in range(B)]
+        scale_col = keep.tile([P, 4], F32, name="scale_col")
+        scale_row = keep.tile([P, D], F32, name="scale_row")
+        w_raw = keep.tile([P, 2 * D], U8, name="w_raw", align_bytes=64)
+        w_raw_plane = keep.tile([P, D], U8, name="w_raw_plane", align_bytes=64)
+        w = keep.tile([P, 2 * D], U8, name="w", align_bytes=64)
+        w_plane = keep.tile([P, D], U8, name="w_plane", align_bytes=64)
+        ident = keep.tile([P, P], F32, name="ident")
+        warm = keep.tile([P, 2], F32, name="warm")
+        zeros = keep.tile([P, P], F32, name="zeros")
+
+        x1_view = x1.rearrange("b (p c) k -> b p (c k)", c=4)
+        x2_view = x2_bytes.rearrange("b (p c) k -> b p (c k)", c=4)
+        out_view = out.rearrange("b (p c) n -> b p c n", c=4)
+
+        def load(tiles, view, b, halves):
+            cols = slice(2 * D * halves[0], 2 * D * (halves[-1] + 1))
+            nc.sync.dma_start(out=tiles[b][:, cols], in_=view[b, :, cols])
+
+        def half(tiles, i):
+            b, j = divmod(i, 2)
+            return tiles[b][:, 2 * D * j : 2 * D * (j + 1)]
+
+        nc.vector.memset(w_raw_plane[:].bitcast(I32), 0)
+        nc.vector.memset(zeros[:], 0.0)
+        nc.vector.memset(warm[:], 0.0)
+        nc.scalar.dma_start(out=scale_col[:], in_=x2_scale.rearrange("a o (p t) -> p (a o t)", t=4))
+        nc.scalar.copy(out=warm[:, 0:1], in_=warm[:, 1:2])
+        nc.sync.dma_start(out=w_raw[:].bitcast(I32), in_=w_words.rearrange("g p n -> p (g n)").bitcast(I32))
+        load(x1_raw, x1_view, 0, (0,))
+        load(x2_raw, x2_view, 0, (0,))
+        load(x1_raw, x1_view, 0, (1,))
+        for q in range(4):
+            nc.sync.dma_start(out=w_raw_plane[32 * q : 32 * q + 4, :].bitcast(I32), in_=w_scales[0, 4 * q : 4 * q + 4, :].bitcast(I32))
+        load(x2_raw, x2_view, 0, (1,))
+        load(x2_raw, x2_view, 1, (0, 1))
+        load(x1_raw, x1_view, 1, (0, 1))
+        load(x2_raw, x2_view, 2, (0, 1))
+        load(x1_raw, x1_view, 2, (0, 1))
+        make_identity(nc, ident[:])
+
+        idle = psum.tile([P, P], F32, name="idle", tag="sim_acc", bufs=BANKS["sim"])
+
+        def busy(count):
+            for k in range(count):
+                nc.tensor.matmul(out=idle[:], lhsT=zeros[:], rhs=zeros[:], start=True, stop=True)
+
+        busy(4)
+
+        spread = psum.tile([P, 4, P], F32, name="spread", tag="x2_turned", bufs=BANKS["x2"])
+        for t in range(4):
+            nc.tensor.transpose(spread[:, t, :], scale_col[:, t : t + 1].to_broadcast([P, P]), ident[:])
+        nc.scalar.copy(out=scale_row[:].rearrange("p (n t) -> p n t", t=4), in_=spread[:].rearrange("p t n -> p n t"))
+
+        turned, k_first, x1_q, h_acc, h, h_q, x2_rows, sums = {}, {}, {}, {}, {}, {}, {}, {}
+
+        def fits(name, i):
+            return nc.vector.tensor_copy if (name, i) in ON_VECTOR else nc.scalar.copy
+
+        def turn(name, i, rows):
+            words = rows.bitcast(F32)
+            acc = psum.tile([P, 2, 2, P], F32, name=name + "_turned", tag=name + "_turned", bufs=BANKS[name])
+            for c in range(2):
+                for u in range(2):
+                    nc.tensor.transpose(acc[:, u, c, :], words[:, 256 * c + u : 256 * (c + 1) : 2], ident[:])
+            turned[name, i] = acc
+
+        def interleave(name, i, stage):
+            out_tile = work.tile([P, HROWS * 4], BF16, name=name + "_k", tag=name + "_k", align_bytes=64)
+            fits(stage, i)(
+                out=out_tile[:].bitcast(F32).rearrange("p (r u) -> p r u", u=2),
+                in_=turned[name, i][:].rearrange("p u c r -> p (c r) u"),
+            )
+            k_first[name, i] = out_tile
+
+        def quantize(rows, name):
+            words = work.tile([P, HROWS], U32, name=name + "_w", tag=name + "_w", align_bytes=64)
+            plane = work.tile([P, HROWS], U8, name=name + "_s", tag=name + "_s", align_bytes=64)
+            nc.vector.quantize_mx(out=words[:].bitcast(FP8X4), scales=plane[:], in_=rows[:])
+            return words, plane
+
+        def stage_W(i):
+            if i == 0:
+                nc.vector.tensor_copy(out=w[:].rearrange("p (t m e) -> p t m e", t=4, e=2), in_=w_raw[:].rearrange("p (m t e) -> p t m e", t=4, e=2))
+
+        def stage_Wp(i):
+            if i == 0:
+                nc.vector.tensor_copy(out=w_plane[:].rearrange("p (t m) -> p t m", t=4), in_=w_raw_plane[:].rearrange("p (m t) -> p t m", t=4))
+
+        def stage_T1(i):
+            turn("x1", i, half(x1_raw, i))
+
+        def stage_C1(i):
+            interleave("x1", i, "C1")
+
+        def stage_Q1(i):
+            x1_q[i] = quantize(k_first["x1", i], "x1")
+
+        def stage_P(i):
+            rows = work.tile([P, 2 * D], BF16, name="x2_rows", tag="x2_rows")
+            for c in range(2):
+                cols = slice(D * c, D * (c + 1))
+                nc.vector.tensor_tensor(out=rows[:, cols], in0=half(x2_raw, i)[:, cols].bitcast(E4M3), in1=scale_row[:], op=MULT)
+            x2_rows[i] = rows
+
+        def stage_T2(i):
+            turn("x2", i, x2_rows[i][:])
+
+        def stage_C2(i):
+            interleave("x2", i, "C2")
+
+        def stage_Q2(i):
+            b, j = divmod(i, 2)
+            cols = slice(HROWS * j, HROWS * (j + 1))
+            nc.vector.quantize_mx(out=x2_words[b][:, cols].bitcast(FP8X4), scales=x2_planes[b][:, cols], in_=k_first["x2", i][:])
+
+        def stage_H(i):
+            words, plane = x1_q[i]
+            for c in range(2):
+                rows = slice(P * c, P * (c + 1))
+                acc = psum.tile([P, 4, P], F32, name="h_acc", tag="h_acc", bufs=BANKS["h"])
+                for t in range(4):
+                    nc.tensor.matmul_mx(
+                        out=acc[:, t, :],
+                        lhsT=w[:, 256 * t : 256 * (t + 1)].bitcast(FP4X4),
+                        lhsT_scale=w_plane[:, P * t : P * (t + 1)],
+                        rhs=words[:, rows].bitcast(FP8X4),
+                        rhs_scale=plane[:, rows],
+                        start=True,
+                        stop=True,
+                    )
+                h_acc[i, c] = acc
+
+        def h_out(i, c, stage):
+            if c == 0:
+                h_tile = work.tile([P, HROWS * 4], BF16, name="h", tag="h", align_bytes=64)
+                h[i] = h_tile
+            fits(stage, i)(
+                out=h[i][:, 512 * c : 512 * (c + 1)].rearrange("p (r t) -> p r t", t=4),
+                in_=h_acc[i, c][:].rearrange("p t r -> p r t"),
+            )
+
+        def stage_HC0(i):
+            h_out(i, 0, "HC0")
+
+        def stage_HC1(i):
+            h_out(i, 1, "HC1")
+
+        def stage_HQ(i):
+            h_q[i] = quantize(h[i], "h")
+
+        def stage_K(i):
+            busy(FILL.get(i, 0))
+
+        def stage_O(i):
+            b = i // 2
+            words, plane = h_q[i]
+            for c in range(2):
+                rows = slice(P * c, P * (c + 1))
+                acc = psum.tile([P, L], F32, name="sim_acc", tag="sim_acc", bufs=BANKS["sim"])
+                nc.tensor.matmul_mx(
+                    out=acc[:],
+                    lhsT=words[:, rows].bitcast(FP8X4),
+                    lhsT_scale=plane[:, rows],
+                    rhs=x2_words[b][:].bitcast(FP8X4),
+                    rhs_scale=x2_planes[b][:],
+                    start=True,
+                    stop=True,
+                )
+                sums[i, c] = acc
+
+        def sim_out(i, c, stage):
+            b, j = divmod(i, 2)
+            result = work.tile([P, L], F32, name="result", tag="result", bufs=12)
+            fits(stage, i)(out=result[:].rearrange("p (m c) -> p m c", c=4), in_=sums[i, c][:].rearrange("p (c m) -> p m c", c=4))
+            nc.sync.dma_start(out=out_view[b, :, 2 * j + c, :], in_=result[:])
+
+        def stage_OC0(i):
+            sim_out(i, 0, "OC0")
+
+        def stage_OC1(i):
+            sim_out(i, 1, "OC1")
+
+        order = (
+            (stage_T1, 0),
+            (stage_HC0, 2),
+            (stage_W, 0),
+            (stage_OC1, 4),
+            (stage_P, 0),
+            (stage_HC1, 2),
+            (stage_C1, 0),
+            (stage_Wp, 0),
+            (stage_T2, 1),
+            (stage_K, 0),
+            (stage_O, 3),
+            (stage_C2, 1),
+            (stage_H, 1),
+            (stage_HQ, 2),
+            (stage_Q1, 0),
+            (stage_Q2, 1),
+            (stage_OC0, 3),
+        )
+        for step in range(HALVES + max(lag for stage, lag in order)):
+            for stage, lag in order:
+                if 0 <= step - lag < HALVES:
+                    stage(step - lag)

@@ -18,7 +18,6 @@ FP4X4 = mybir.dt.float4_e2m1fn_x4
 MULT = mybir.AluOpType.mult
 
 HALVES = 2 * B
-FILL = {0: 2, 1: 1, 2: 2}
 BANKS = {"x1": 1, "x2": 2, "h": 2, "sim": 3}
 ON_VECTOR = (("C2", 3), ("C2", 5), ("HC0", 2), ("HC0", 3), ("HC1", 5), ("OC0", 5), ("OC1", 4),)
 HROWS = 256
@@ -43,8 +42,6 @@ def tile_coattentionandcombine_pa_w4_kernel(tc, x1, w_words, w_scales, x2_bytes,
         w = keep.tile([P, 2 * D], U8, name="w", align_bytes=64)
         w_plane = keep.tile([P, D], U8, name="w_plane", align_bytes=64)
         ident = keep.tile([P, P], F32, name="ident")
-        warm = keep.tile([P, 2], F32, name="warm")
-        zeros = keep.tile([P, P], F32, name="zeros")
 
         x1_view = x1.rearrange("b (p c) k -> b p (c k)", c=4)
         x2_view = x2_bytes.rearrange("b (p c) k -> b p (c k)", c=4)
@@ -59,10 +56,7 @@ def tile_coattentionandcombine_pa_w4_kernel(tc, x1, w_words, w_scales, x2_bytes,
             return tiles[b][:, 2 * D * j : 2 * D * (j + 1)]
 
         nc.vector.memset(w_raw_plane[:].bitcast(I32), 0)
-        nc.vector.memset(zeros[:], 0.0)
-        nc.vector.memset(warm[:], 0.0)
         nc.scalar.dma_start(out=scale_col[:], in_=x2_scale.rearrange("a o (p t) -> p (a o t)", t=4))
-        nc.scalar.copy(out=warm[:, 0:1], in_=warm[:, 1:2])
         nc.sync.dma_start(out=w_raw[:].bitcast(I32), in_=w_words.rearrange("g p n -> p (g n)").bitcast(I32))
         load(x1_raw, x1_view, 0, (0,))
         load(x2_raw, x2_view, 0, (0,))
@@ -75,14 +69,6 @@ def tile_coattentionandcombine_pa_w4_kernel(tc, x1, w_words, w_scales, x2_bytes,
         load(x2_raw, x2_view, 2, (0, 1))
         load(x1_raw, x1_view, 2, (0, 1))
         make_identity(nc, ident[:])
-
-        idle = psum.tile([P, P], F32, name="idle", tag="sim_acc", bufs=BANKS["sim"])
-
-        def busy(count):
-            for k in range(count):
-                nc.tensor.matmul(out=idle[:], lhsT=zeros[:], rhs=zeros[:], start=True, stop=True)
-
-        busy(4)
 
         spread = psum.tile([P, 4, P], F32, name="spread", tag="x2_turned", bufs=BANKS["x2"])
         for t in range(4):
@@ -186,9 +172,6 @@ def tile_coattentionandcombine_pa_w4_kernel(tc, x1, w_words, w_scales, x2_bytes,
         def stage_HQ(i):
             h_q[i] = quantize(h[i], "h")
 
-        def stage_K(i):
-            busy(FILL.get(i, 0))
-
         def stage_O(i):
             b = i // 2
             words, plane = h_q[i]
@@ -228,7 +211,6 @@ def tile_coattentionandcombine_pa_w4_kernel(tc, x1, w_words, w_scales, x2_bytes,
             (stage_C1, 0),
             (stage_Wp, 0),
             (stage_T2, 1),
-            (stage_K, 0),
             (stage_O, 3),
             (stage_C2, 1),
             (stage_H, 1),

@@ -18,130 +18,139 @@ FP4X4 = mybir.dt.float4_e2m1fn_x4
 MULT = mybir.AluOpType.mult
 
 HALVES = 2 * B
-BANKS = {"x1": 1, "x2": 2, "h": 2, "sim": 3}
-ON_VECTOR = (("C2", 3), ("C2", 5), ("HC0", 2), ("HC0", 3), ("HC1", 5), ("OC0", 5), ("OC1", 4),)
-HROWS = 256
+ROWS = 256
+BANKS = 8
+WIDE_ON_SCALAR = 4
 
 
 def tile_coattentionandcombine_pa_w4_kernel(tc, x1, w_words, w_scales, x2_bytes, x2_scale, out):
     nc = tc.nc
     with ExitStack() as ctx:
         keep = ctx.enter_context(tc.tile_pool(name="keep", bufs=1))
-        work = ctx.enter_context(tc.tile_pool(name="work", bufs=6))
+        work = ctx.enter_context(tc.tile_pool(name="work", bufs=3))
         psum = ctx.enter_context(tc.psum_pool(name="psum", bufs=2))
         ctx.enter_context(tc.manual_schedule())
 
-        x1_raw = [keep.tile([P, 4 * D], BF16, name="x1_raw%d" % b) for b in range(B)]
-        x2_raw = [keep.tile([P, 4 * D], U8, name="x2_raw%d" % b) for b in range(B)]
+        x1_raw = [keep.tile([P, 2 * D], BF16, name="x1_raw%d" % i) for i in range(HALVES)]
+        x2_raw = [keep.tile([P, 2 * D], U8, name="x2_raw%d" % i) for i in range(HALVES)]
         x2_words = [keep.tile([P, L], U32, name="x2_words%d" % b, align_bytes=64) for b in range(B)]
         x2_planes = [keep.tile([P, L], U8, name="x2_planes%d" % b, align_bytes=64) for b in range(B)]
         scale_col = keep.tile([P, 4], F32, name="scale_col")
-        scale_row = keep.tile([P, D], F32, name="scale_row")
+        ones = keep.tile([P, 1], F32, name="ones")
         w_raw = keep.tile([P, 2 * D], U8, name="w_raw", align_bytes=64)
         w_raw_plane = keep.tile([P, D], U8, name="w_raw_plane", align_bytes=64)
         w = keep.tile([P, 2 * D], U8, name="w", align_bytes=64)
         w_plane = keep.tile([P, D], U8, name="w_plane", align_bytes=64)
         ident = keep.tile([P, P], F32, name="ident")
+        zeros = keep.tile([P, P], F32, name="zeros")
 
-        x1_view = x1.rearrange("b (p c) k -> b p (c k)", c=4)
-        x2_view = x2_bytes.rearrange("b (p c) k -> b p (c k)", c=4)
+        x1_view = x1.rearrange("b (p j c) k -> b j p (c k)", j=2, c=2)
+        x2_view = x2_bytes.rearrange("b (p j c) k -> b j p (c k)", j=2, c=2)
         out_view = out.rearrange("b (p c) n -> b p c n", c=4)
 
-        def load(tiles, view, b, halves):
-            cols = slice(2 * D * halves[0], 2 * D * (halves[-1] + 1))
-            nc.sync.dma_start(out=tiles[b][:, cols], in_=view[b, :, cols])
+        def load_x1(i):
+            nc.sync.dma_start(out=x1_raw[i][:], in_=x1_view[i // 2, i % 2])
 
-        def half(tiles, i):
-            b, j = divmod(i, 2)
-            return tiles[b][:, 2 * D * j : 2 * D * (j + 1)]
+        def load_x2(i):
+            nc.sync.dma_start(out=x2_raw[i][:], in_=x2_view[i // 2, i % 2])
 
+        nc.vector.memset(zeros[:], 0.0)
         nc.vector.memset(w_raw_plane[:].bitcast(I32), 0)
-        nc.scalar.dma_start(out=scale_col[:], in_=x2_scale.rearrange("a o (p t) -> p (a o t)", t=4))
+        nc.vector.memset(ones[:], 1.0)
+        load_x1(0)
+        load_x2(0)
         nc.sync.dma_start(out=w_raw[:].bitcast(I32), in_=w_words.rearrange("g p n -> p (g n)").bitcast(I32))
-        load(x1_raw, x1_view, 0, (0,))
-        load(x2_raw, x2_view, 0, (0,))
-        load(x1_raw, x1_view, 0, (1,))
+        load_x2(1)
         for q in range(4):
             nc.sync.dma_start(out=w_raw_plane[32 * q : 32 * q + 4, :].bitcast(I32), in_=w_scales[0, 4 * q : 4 * q + 4, :].bitcast(I32))
-        load(x2_raw, x2_view, 0, (1,))
-        load(x2_raw, x2_view, 1, (0, 1))
-        load(x1_raw, x1_view, 1, (0, 1))
-        load(x2_raw, x2_view, 2, (0, 1))
-        load(x1_raw, x1_view, 2, (0, 1))
+        nc.sync.dma_start(out=scale_col[:], in_=x2_scale.rearrange("a o (p t) -> p (a o t)", t=4))
+        load_x1(1)
+        for i in range(2, HALVES):
+            load_x2(i)
+            load_x1(i)
         make_identity(nc, ident[:])
 
-        spread = psum.tile([P, 4, P], F32, name="spread", tag="x2_turned", bufs=BANKS["x2"])
-        for t in range(4):
-            nc.tensor.transpose(spread[:, t, :], scale_col[:, t : t + 1].to_broadcast([P, P]), ident[:])
-        nc.scalar.copy(out=scale_row[:].rearrange("p (n t) -> p n t", t=4), in_=spread[:].rearrange("p t n -> p n t"))
-
-        turned, k_first, x1_q, h_acc, h, h_q, x2_rows, sums = {}, {}, {}, {}, {}, {}, {}, {}
-
-        def fits(name, i):
-            return nc.vector.tensor_copy if (name, i) in ON_VECTOR else nc.scalar.copy
-
-        def turn(name, i, rows):
-            words = rows.bitcast(F32)
-            acc = psum.tile([P, 2, 2, P], F32, name=name + "_turned", tag=name + "_turned", bufs=BANKS[name])
-            for c in range(2):
-                for u in range(2):
-                    nc.tensor.transpose(acc[:, u, c, :], words[:, 256 * c + u : 256 * (c + 1) : 2], ident[:])
-            turned[name, i] = acc
-
-        def interleave(name, i, stage):
-            out_tile = work.tile([P, HROWS * 4], BF16, name=name + "_k", tag=name + "_k", align_bytes=64)
-            fits(stage, i)(
-                out=out_tile[:].bitcast(F32).rearrange("p (r u) -> p r u", u=2),
-                in_=turned[name, i][:].rearrange("p u c r -> p (c r) u"),
-            )
-            k_first[name, i] = out_tile
+        wide, turned, k_first, x1_q, h_acc, h, h_q, sums = {}, {}, {}, {}, {}, {}, {}, {}
 
         def quantize(rows, name):
-            words = work.tile([P, HROWS], U32, name=name + "_w", tag=name + "_w", align_bytes=64)
-            plane = work.tile([P, HROWS], U8, name=name + "_s", tag=name + "_s", align_bytes=64)
+            words = work.tile([P, ROWS], U32, name=name + "_words", tag=name + "_words", align_bytes=64)
+            plane = work.tile([P, ROWS], U8, name=name + "_plane", tag=name + "_plane", align_bytes=64)
             nc.vector.quantize_mx(out=words[:].bitcast(FP8X4), scales=plane[:], in_=rows[:])
             return words, plane
 
-        def stage_W(i):
-            if i == 0:
-                nc.vector.tensor_copy(out=w[:].rearrange("p (t m e) -> p t m e", t=4, e=2), in_=w_raw[:].rearrange("p (m t e) -> p t m e", t=4, e=2))
+        def order_w():
+            nc.vector.tensor_copy(out=w[:].rearrange("p (t m e) -> p t m e", t=4, e=2), in_=w_raw[:].rearrange("p (m t e) -> p t m e", t=4, e=2))
 
-        def stage_Wp(i):
-            if i == 0:
-                nc.vector.tensor_copy(out=w_plane[:].rearrange("p (t m) -> p t m", t=4), in_=w_raw_plane[:].rearrange("p (m t) -> p t m", t=4))
+        def order_w_plane():
+            nc.vector.tensor_copy(out=w_plane[:].rearrange("p (t m) -> p t m", t=4), in_=w_raw_plane[:].rearrange("p (m t) -> p t m", t=4))
 
-        def stage_T1(i):
-            turn("x1", i, half(x1_raw, i))
+        def widen(i, blocks, on_vector):
+            count = len(blocks)
+            rows = work.tile([P, count * D], BF16, name="x2_wide", tag="x2_wide")
+            codes = x2_raw[i][:, D * blocks[0] : D * (blocks[-1] + 1)].bitcast(E4M3)
+            words = rows[:].bitcast(F32)
+            if on_vector:
+                nc.vector.tensor_scalar(
+                    out=rows[:].rearrange("p (u m e) -> p m u e", u=2, e=2),
+                    in0=codes.rearrange("p (m u e) -> p m u e", u=2, e=2),
+                    scalar1=ones[:],
+                    scalar2=None,
+                    op0=MULT,
+                )
+            else:
+                nc.scalar.copy(out=rows[:], in_=codes)
+            for n, c in enumerate(blocks):
+                for u in range(2):
+                    if on_vector:
+                        wide[i, c, u] = words[:, P * (count * u + n) : P * (count * u + n + 1)]
+                    else:
+                        wide[i, c, u] = words[:, 256 * n + u : 256 * (n + 1) : 2]
 
-        def stage_C1(i):
-            interleave("x1", i, "C1")
+        def turn(name, i, parts):
+            acc = psum.tile([P, 2, 2, P], F32, name=name + "_turned", tag="bank", bufs=BANKS)
+            for c in range(2):
+                for u in range(2):
+                    nc.tensor.transpose(acc[:, u, c, :], parts[c, u], ident[:])
+            turned[name, i] = acc
 
-        def stage_Q1(i):
+        def turn_x1(i):
+            words = x1_raw[i][:].bitcast(F32)
+            turn("x1", i, dict(((c, u), words[:, 256 * c + u : 256 * (c + 1) : 2]) for c in range(2) for u in range(2)))
+
+        def turn_x2(i):
+            turn("x2", i, dict(((c, u), wide[i, c, u]) for c in range(2) for u in range(2)))
+
+        def empty_x1(i):
+            rows = work.tile([P, ROWS * 4], BF16, name="x1_k", tag="x1_k", align_bytes=64)
+            nc.scalar.copy(
+                out=rows[:].bitcast(F32).rearrange("p (r u) -> p r u", u=2),
+                in_=turned["x1", i][:].rearrange("p u c r -> p (c r) u"),
+            )
+            k_first["x1", i] = rows
+
+        def scale_x2(i):
+            rows = work.tile([P, ROWS * 4], BF16, name="x2_k", tag="x2_k", align_bytes=64)
+            nc.vector.tensor_tensor(
+                out=rows[:].rearrange("p (r u e) -> p r u e", u=2, e=2),
+                in0=turned["x2", i][:].rearrange("p u c r -> p (u c r)").bitcast(BF16).rearrange("p (u r e) -> p r u e", u=2, e=2),
+                in1=scale_col[:].rearrange("p (u e) -> p u e", u=2).unsqueeze(1).to_broadcast([P, ROWS, 2, 2]),
+                op=MULT,
+            )
+            k_first["x2", i] = rows
+
+        def quantize_x1(i):
             x1_q[i] = quantize(k_first["x1", i], "x1")
 
-        def stage_P(i):
-            rows = work.tile([P, 2 * D], BF16, name="x2_rows", tag="x2_rows")
-            for c in range(2):
-                cols = slice(D * c, D * (c + 1))
-                nc.vector.tensor_tensor(out=rows[:, cols], in0=half(x2_raw, i)[:, cols].bitcast(E4M3), in1=scale_row[:], op=MULT)
-            x2_rows[i] = rows
-
-        def stage_T2(i):
-            turn("x2", i, x2_rows[i][:])
-
-        def stage_C2(i):
-            interleave("x2", i, "C2")
-
-        def stage_Q2(i):
+        def quantize_x2(i):
             b, j = divmod(i, 2)
-            cols = slice(HROWS * j, HROWS * (j + 1))
+            cols = slice(ROWS * j, ROWS * (j + 1))
             nc.vector.quantize_mx(out=x2_words[b][:, cols].bitcast(FP8X4), scales=x2_planes[b][:, cols], in_=k_first["x2", i][:])
 
-        def stage_H(i):
+        def project(i):
             words, plane = x1_q[i]
             for c in range(2):
                 rows = slice(P * c, P * (c + 1))
-                acc = psum.tile([P, 4, P], F32, name="h_acc", tag="h_acc", bufs=BANKS["h"])
+                acc = psum.tile([P, 4, P], F32, name="h_acc", tag="bank", bufs=BANKS)
                 for t in range(4):
                     nc.tensor.matmul_mx(
                         out=acc[:, t, :],
@@ -154,30 +163,33 @@ def tile_coattentionandcombine_pa_w4_kernel(tc, x1, w_words, w_scales, x2_bytes,
                     )
                 h_acc[i, c] = acc
 
-        def h_out(i, c, stage):
+        def empty_h(i, c, copy):
             if c == 0:
-                h_tile = work.tile([P, HROWS * 4], BF16, name="h", tag="h", align_bytes=64)
+                h_tile = work.tile([P, ROWS * 4], BF16, name="h", tag="h", align_bytes=64)
                 h[i] = h_tile
-            fits(stage, i)(
+            copy(
                 out=h[i][:, 512 * c : 512 * (c + 1)].rearrange("p (r t) -> p r t", t=4),
                 in_=h_acc[i, c][:].rearrange("p t r -> p r t"),
             )
 
-        def stage_HC0(i):
-            h_out(i, 0, "HC0")
-
-        def stage_HC1(i):
-            h_out(i, 1, "HC1")
-
-        def stage_HQ(i):
+        def quantize_h(i):
             h_q[i] = quantize(h[i], "h")
 
-        def stage_O(i):
+        def quantize_h_block(i, c):
+            if c == 0:
+                words = work.tile([P, ROWS], U32, name="h_words", tag="h_words", align_bytes=64)
+                plane = work.tile([P, ROWS], U8, name="h_plane", tag="h_plane", align_bytes=64)
+                h_q[i] = words, plane
+            words, plane = h_q[i]
+            rows = slice(P * c, P * (c + 1))
+            nc.vector.quantize_mx(out=words[:, rows].bitcast(FP8X4), scales=plane[:, rows], in_=h[i][:, 512 * c : 512 * (c + 1)])
+
+        def compare(i, blocks=(0, 1)):
             b = i // 2
             words, plane = h_q[i]
-            for c in range(2):
+            for c in blocks:
                 rows = slice(P * c, P * (c + 1))
-                acc = psum.tile([P, L], F32, name="sim_acc", tag="sim_acc", bufs=BANKS["sim"])
+                acc = psum.tile([P, L], F32, name="sim_acc", tag="bank", bufs=BANKS)
                 nc.tensor.matmul_mx(
                     out=acc[:],
                     lhsT=words[:, rows].bitcast(FP8X4),
@@ -189,37 +201,71 @@ def tile_coattentionandcombine_pa_w4_kernel(tc, x1, w_words, w_scales, x2_bytes,
                 )
                 sums[i, c] = acc
 
-        def sim_out(i, c, stage):
+        def empty_sim(i, c, copy):
             b, j = divmod(i, 2)
-            result = work.tile([P, L], F32, name="result", tag="result", bufs=12)
-            fits(stage, i)(out=result[:].rearrange("p (m c) -> p m c", c=4), in_=sums[i, c][:].rearrange("p (c m) -> p m c", c=4))
+            result = work.tile([P, L], F32, name="result", tag="result", bufs=2 * HALVES)
+            copy(out=result[:].rearrange("p (m c) -> p m c", c=4), in_=sums[i, c][:].rearrange("p (c m) -> p m c", c=4))
             nc.sync.dma_start(out=out_view[b, :, 2 * j + c, :], in_=result[:])
 
-        def stage_OC0(i):
-            sim_out(i, 0, "OC0")
+        idle = psum.tile([P, P], F32, name="idle", tag="bank", bufs=BANKS)
 
-        def stage_OC1(i):
-            sim_out(i, 1, "OC1")
+        def warm(count):
+            for k in range(count):
+                nc.tensor.matmul(out=idle[:], lhsT=zeros[:], rhs=zeros[:], start=True, stop=True)
 
-        order = (
-            (stage_T1, 0),
-            (stage_HC0, 2),
-            (stage_W, 0),
-            (stage_OC1, 4),
-            (stage_P, 0),
-            (stage_HC1, 2),
-            (stage_C1, 0),
-            (stage_Wp, 0),
-            (stage_T2, 1),
-            (stage_O, 3),
-            (stage_C2, 1),
-            (stage_H, 1),
-            (stage_HQ, 2),
-            (stage_Q1, 0),
-            (stage_Q2, 1),
-            (stage_OC0, 3),
-        )
-        for step in range(HALVES + max(lag for stage, lag in order)):
-            for stage, lag in order:
-                if 0 <= step - lag < HALVES:
-                    stage(step - lag)
+        def live(i):
+            return 0 <= i < HALVES
+
+        both = (0, 1)
+        warm(3)
+        turn_x1(0)
+        warm(2)
+        widen(0, both, False)
+        empty_x1(0)
+        order_w()
+        order_w_plane()
+        turn_x2(0)
+        widen(1, both, False)
+        quantize_x1(0)
+        scale_x2(0)
+        last = HALVES - 1
+        for s in range(last):
+            turn_x1(s + 1)
+            turn_x2(s + 1)
+            if s + 2 < WIDE_ON_SCALAR:
+                widen(s + 2, both, False)
+            if live(s - 2):
+                empty_sim(s - 2, 0, nc.scalar.copy)
+            if live(s - 1):
+                quantize_h(s - 1)
+            scale_x2(s + 1)
+            if WIDE_ON_SCALAR <= s + 2 <= last:
+                widen(s + 2, both, True)
+            if live(s - 2) and s < 4:
+                empty_sim(s - 2, 1, nc.scalar.copy)
+            empty_x1(s + 1)
+            project(s)
+            if s == 0:
+                quantize_x2(0)
+            if live(s - 1):
+                compare(s - 1)
+            quantize_x1(s + 1)
+            quantize_x2(s + 1)
+            if live(s - 2) and s >= 4:
+                empty_sim(s - 2, 1, nc.vector.tensor_copy)
+            empty_h(s, 0, nc.scalar.copy)
+            empty_h(s, 1, nc.scalar.copy)
+        project(last)
+        quantize_h(last - 1)
+        empty_sim(last - 2, 0, nc.scalar.copy)
+        empty_h(last, 0, nc.vector.tensor_copy)
+        compare(last - 1)
+        empty_h(last, 1, nc.scalar.copy)
+        empty_sim(last - 2, 1, nc.vector.tensor_copy)
+        quantize_h_block(last, 0)
+        empty_sim(last - 1, 0, nc.scalar.copy)
+        quantize_h_block(last, 1)
+        compare(last)
+        empty_sim(last - 1, 1, nc.vector.tensor_copy)
+        empty_sim(last, 0, nc.scalar.copy)
+        empty_sim(last, 1, nc.vector.tensor_copy)

@@ -63,8 +63,8 @@ def tile_coattentionandcombine_pa_w4_kernel(tc, x1, w_words, w_scales, x2_bytes,
         load_x2(1)
         for q in range(4):
             nc.sync.dma_start(out=w_raw_plane[32 * q : 32 * q + 4, :].bitcast(I32), in_=w_scales[0, 4 * q : 4 * q + 4, :].bitcast(I32))
-        nc.sync.dma_start(out=scale_col[:], in_=x2_scale.rearrange("a o (p t) -> p (a o t)", t=4))
         load_x1(1)
+        nc.sync.dma_start(out=scale_col[:], in_=x2_scale.rearrange("a o (p t) -> p (a o t)", t=4))
         for i in range(2, HALVES):
             load_x2(i)
             load_x1(i)
@@ -86,7 +86,7 @@ def tile_coattentionandcombine_pa_w4_kernel(tc, x1, w_words, w_scales, x2_bytes,
 
         def widen(i, blocks, on_vector):
             count = len(blocks)
-            rows = work.tile([P, count * D], BF16, name="x2_wide", tag="x2_wide")
+            rows = work.tile([P, count * D], BF16, name="x2_wide", tag="x2_wide", bufs=4)
             codes = x2_raw[i][:, D * blocks[0] : D * (blocks[-1] + 1)].bitcast(E4M3)
             words = rows[:].bitcast(F32)
             if on_vector:
@@ -217,53 +217,56 @@ def tile_coattentionandcombine_pa_w4_kernel(tc, x1, w_words, w_scales, x2_bytes,
             return 0 <= i < HALVES
 
         both = (0, 1)
+        last = HALVES - 1
         warm(3)
         turn_x1(0)
         warm(2)
-        widen(0, both, False)
+        widen(0, both, True)
         empty_x1(0)
         order_w()
         order_w_plane()
         turn_x2(0)
+        warm(0)
         widen(1, both, False)
         quantize_x1(0)
         scale_x2(0)
-        last = HALVES - 1
+        widen(2, both, False)
         for s in range(last):
             turn_x1(s + 1)
             turn_x2(s + 1)
-            if s + 2 < WIDE_ON_SCALAR:
-                widen(s + 2, both, False)
             if live(s - 2):
-                empty_sim(s - 2, 0, nc.scalar.copy)
-            if live(s - 1):
-                quantize_h(s - 1)
-            scale_x2(s + 1)
-            if WIDE_ON_SCALAR <= s + 2 <= last:
-                widen(s + 2, both, True)
-            if live(s - 2) and s < 4:
                 empty_sim(s - 2, 1, nc.scalar.copy)
+            scale_x2(s + 1)
             empty_x1(s + 1)
-            project(s)
             if s == 0:
+                widen(3, both, False)
                 quantize_x2(0)
+            project(s)
             if live(s - 1):
                 compare(s - 1)
             quantize_x1(s + 1)
             quantize_x2(s + 1)
-            if live(s - 2) and s >= 4:
-                empty_sim(s - 2, 1, nc.vector.tensor_copy)
+            if s > 0 and live(s + 3) and (s > 0):
+                widen(s + 3, both, True)
+            if live(s - 1) and s + 1 < last and (s > 2):
+                empty_sim(s - 1, 0, nc.vector.tensor_copy)
             empty_h(s, 0, nc.scalar.copy)
             empty_h(s, 1, nc.scalar.copy)
+            if s > 0 and live(s + 3) and not (s > 0):
+                widen(s + 3, both, False)
+            if live(s - 1) and s + 1 < last and not (s > 2):
+                empty_sim(s - 1, 0, nc.scalar.copy)
+            if s + 1 < last:
+                quantize_h(s)
         project(last)
+        empty_sim(last - 2, 0, nc.vector.tensor_copy)
         quantize_h(last - 1)
-        empty_sim(last - 2, 0, nc.scalar.copy)
-        empty_h(last, 0, nc.vector.tensor_copy)
         compare(last - 1)
-        empty_h(last, 1, nc.scalar.copy)
-        empty_sim(last - 2, 1, nc.vector.tensor_copy)
-        quantize_h_block(last, 0)
+        empty_sim(last - 2, 1, nc.scalar.copy)
+        empty_h(last, 0, nc.scalar.copy)
+        empty_h(last, 1, nc.vector.tensor_copy)
         empty_sim(last - 1, 0, nc.scalar.copy)
+        quantize_h_block(last, 0)
         quantize_h_block(last, 1)
         compare(last)
         empty_sim(last - 1, 1, nc.vector.tensor_copy)

@@ -12,6 +12,7 @@ BF16 = mybir.dt.bfloat16
 I32 = mybir.dt.int32
 U32 = mybir.dt.uint32
 U8 = mybir.dt.uint8
+U16 = mybir.dt.uint16
 E4M3 = mybir.dt.float8_e4m3fn
 FP8X4 = mybir.dt.float8_e4m3fn_x4
 FP4X4 = mybir.dt.float4_e2m1fn_x4
@@ -57,6 +58,7 @@ def tile_coattentionandcombine_pa_w4_kernel(tc, x1, w_words, w_scales, x2_bytes,
         nc.vector.memset(zeros[:], 0.0)
         nc.vector.memset(w_raw_plane[:].bitcast(I32), 0)
         nc.vector.memset(ones[:], 1.0)
+        nc.scalar.dma_start(out=scale_col[:], in_=x2_scale.rearrange("a o (p t) -> p (a o t)", t=4))
         load_x1(0)
         load_x2(0)
         nc.sync.dma_start(out=w_raw[:].bitcast(I32), in_=w_words.rearrange("g p n -> p (g n)").bitcast(I32))
@@ -64,7 +66,6 @@ def tile_coattentionandcombine_pa_w4_kernel(tc, x1, w_words, w_scales, x2_bytes,
         for q in range(4):
             nc.sync.dma_start(out=w_raw_plane[32 * q : 32 * q + 4, :].bitcast(I32), in_=w_scales[0, 4 * q : 4 * q + 4, :].bitcast(I32))
         load_x1(1)
-        nc.sync.dma_start(out=scale_col[:], in_=x2_scale.rearrange("a o (p t) -> p (a o t)", t=4))
         for i in range(2, HALVES):
             load_x2(i)
             load_x1(i)
@@ -79,7 +80,7 @@ def tile_coattentionandcombine_pa_w4_kernel(tc, x1, w_words, w_scales, x2_bytes,
             return words, plane
 
         def order_w():
-            nc.vector.tensor_copy(out=w[:].rearrange("p (t m e) -> p t m e", t=4, e=2), in_=w_raw[:].rearrange("p (m t e) -> p t m e", t=4, e=2))
+            nc.vector.tensor_copy(out=w[:].bitcast(U16).rearrange("p (t m) -> p t m", t=4), in_=w_raw[:].bitcast(U16).rearrange("p (m t) -> p t m", t=4))
 
         def order_w_plane():
             nc.vector.tensor_copy(out=w_plane[:].rearrange("p (t m) -> p t m", t=4), in_=w_raw_plane[:].rearrange("p (m t) -> p t m", t=4))

@@ -221,41 +221,40 @@ def tile_coattentionandcombine_pa_w4_kernel(tc, x1, w_words, w_scales, x2_bytes,
         last = HALVES - 1
         warm(3)
         turn_x1(0)
-        warm(2)
+        warm(1)
         widen(0, both, True)
+        widen(1, both, False)
         empty_x1(0)
         order_w()
         order_w_plane()
         turn_x2(0)
-        warm(0)
-        widen(1, both, False)
-        quantize_x1(0)
+        warm(2)
         scale_x2(0)
-        widen(2, both, False)
+        quantize_x1(0)
+        quantize_x2(0)
         for s in range(last):
             turn_x1(s + 1)
             turn_x2(s + 1)
-            if live(s - 2):
+            if live(s - 2) and s + 1 < last:
                 empty_sim(s - 2, 1, nc.scalar.copy)
             scale_x2(s + 1)
             empty_x1(s + 1)
+            if s + 1 == last:
+                empty_sim(s - 2, 1, nc.scalar.copy)
             if s == 0:
-                widen(3, both, False)
-                quantize_x2(0)
+                widen(2, both, False)
             project(s)
             if live(s - 1):
                 compare(s - 1)
             quantize_x1(s + 1)
             quantize_x2(s + 1)
-            if s > 0 and live(s + 3) and (s > 0):
+            if live(s + 3):
                 widen(s + 3, both, True)
-            if live(s - 1) and s + 1 < last and (s > 2):
+            elif s + 1 < last and False:
                 empty_sim(s - 1, 0, nc.vector.tensor_copy)
             empty_h(s, 0, nc.scalar.copy)
             empty_h(s, 1, nc.scalar.copy)
-            if s > 0 and live(s + 3) and not (s > 0):
-                widen(s + 3, both, False)
-            if live(s - 1) and s + 1 < last and not (s > 2):
+            if live(s - 1) and (live(s + 3) or not False) and s + 1 < last:
                 empty_sim(s - 1, 0, nc.scalar.copy)
             if s + 1 < last:
                 quantize_h(s)

@@ -46,7 +46,7 @@ def tile_coattentionandcombine_pa_w4_kernel(tc, x1, w_words, w_scales, x2_bytes,
         zeros = keep.tile([P, P], F32, name="zeros")
 
         x1_view = x1.rearrange("b (p j c) k -> b j p (c k)", j=2, c=2)
-        x2_view = x2_bytes.rearrange("b (p j c) k -> b j p (c k)", j=2, c=2)
+        x2_view = x2_bytes.rearrange("b (j p c) k -> b j p (c k)", j=2, c=2)
         out_view = out.rearrange("b (p c) n -> b p c n", c=4)
 
         def load_x1(i):
@@ -87,7 +87,7 @@ def tile_coattentionandcombine_pa_w4_kernel(tc, x1, w_words, w_scales, x2_bytes,
 
         def widen(i, blocks, on_vector):
             count = len(blocks)
-            rows = work.tile([P, count * D], BF16, name="x2_wide", tag="x2_wide", bufs=4)
+            rows = work.tile([P, count * D], BF16, name="x2_wide", tag="x2_wide", bufs=6)
             codes = x2_raw[i][:, D * blocks[0] : D * (blocks[-1] + 1)].bitcast(E4M3)
             words = rows[:].bitcast(F32)
             if on_vector:
@@ -185,28 +185,54 @@ def tile_coattentionandcombine_pa_w4_kernel(tc, x1, w_words, w_scales, x2_bytes,
             rows = slice(P * c, P * (c + 1))
             nc.vector.quantize_mx(out=words[:, rows].bitcast(FP8X4), scales=plane[:, rows], in_=h[i][:, 512 * c : 512 * (c + 1)])
 
-        def compare(i, blocks=(0, 1)):
+        def compare(i, blocks=(0, 1), sides=(0, 1)):
             b = i // 2
             words, plane = h_q[i]
+            cols = slice(ROWS * sides[0], ROWS * (sides[-1] + 1))
             for c in blocks:
                 rows = slice(P * c, P * (c + 1))
-                acc = psum.tile([P, L], F32, name="sim_acc", tag="bank", bufs=BANKS)
+                acc = psum.tile([P, ROWS * len(sides)], F32, name="sim_acc", tag="bank", bufs=BANKS)
                 nc.tensor.matmul_mx(
                     out=acc[:],
                     lhsT=words[:, rows].bitcast(FP8X4),
                     lhsT_scale=plane[:, rows],
-                    rhs=x2_words[b][:].bitcast(FP8X4),
-                    rhs_scale=x2_planes[b][:],
+                    rhs=x2_words[b][:, cols].bitcast(FP8X4),
+                    rhs_scale=x2_planes[b][:, cols],
                     start=True,
                     stop=True,
                 )
-                sums[i, c] = acc
+                sums[i, c, sides] = acc
 
-        def empty_sim(i, c, copy):
+        def compare_side(i, side):
+            b = i // 2
+            words, plane = h_q[i]
+            cols = slice(ROWS * side, ROWS * (side + 1))
+            acc = psum.tile([P, 2, ROWS], F32, name="sim_acc", tag="bank", bufs=BANKS)
+            for c in range(2):
+                rows = slice(P * c, P * (c + 1))
+                nc.tensor.matmul_mx(
+                    out=acc[:, c, :],
+                    lhsT=words[:, rows].bitcast(FP8X4),
+                    lhsT_scale=plane[:, rows],
+                    rhs=x2_words[b][:, cols].bitcast(FP8X4),
+                    rhs_scale=x2_planes[b][:, cols],
+                    start=True,
+                    stop=True,
+                )
+            sums[i, side] = acc
+
+        def empty_side(i, side, copy):
             b, j = divmod(i, 2)
-            result = work.tile([P, L], F32, name="result", tag="result", bufs=2 * HALVES)
-            copy(out=result[:].rearrange("p (m c) -> p m c", c=4), in_=sums[i, c][:].rearrange("p (c m) -> p m c", c=4))
-            nc.sync.dma_start(out=out_view[b, :, 2 * j + c, :], in_=result[:])
+            result = work.tile([P, 2, ROWS], F32, name="result", tag="result", bufs=16)
+            copy(out=result[:].rearrange("p c (m e) -> p c m e", e=2), in_=sums[i, side][:].rearrange("p c (e m) -> p c m e", e=2))
+            nc.sync.dma_start(out=out_view[b, :, 2 * j : 2 * j + 2, ROWS * side : ROWS * (side + 1)], in_=result[:])
+
+        def empty_sim(i, c, copy, sides=(0, 1)):
+            b, j = divmod(i, 2)
+            cols = slice(ROWS * sides[0], ROWS * (sides[-1] + 1))
+            result = work.tile([P, ROWS * len(sides)], F32, name="result", tag="result", bufs=16)
+            copy(out=result[:].rearrange("p (s m e) -> p s m e", m=P, e=2), in_=sums[i, c, sides][:].rearrange("p (s e m) -> p s m e", m=P, e=2))
+            nc.sync.dma_start(out=out_view[b, :, 2 * j + c, cols], in_=result[:])
 
         idle = psum.tile([P, P], F32, name="idle", tag="bank", bufs=BANKS)
 
@@ -217,58 +243,93 @@ def tile_coattentionandcombine_pa_w4_kernel(tc, x1, w_words, w_scales, x2_bytes,
         def live(i):
             return 0 <= i < HALVES
 
-        both = (0, 1)
-        last = HALVES - 1
         warm(3)
         turn_x1(0)
         warm(1)
-        widen(0, both, True)
-        widen(1, both, False)
+        widen(0, (0, 1), True)
+        widen(1, (0, 1), False)
         empty_x1(0)
         order_w()
         order_w_plane()
         turn_x2(0)
         warm(2)
+        widen(2, (0, 1), False)
         scale_x2(0)
         quantize_x1(0)
         quantize_x2(0)
-        for s in range(last):
-            turn_x1(s + 1)
-            turn_x2(s + 1)
-            if live(s - 2) and s + 1 < last:
-                empty_sim(s - 2, 1, nc.scalar.copy)
-            scale_x2(s + 1)
-            empty_x1(s + 1)
-            if s + 1 == last:
-                empty_sim(s - 2, 1, nc.scalar.copy)
-            if s == 0:
-                widen(2, both, False)
-            project(s)
-            if live(s - 1):
-                compare(s - 1)
-            quantize_x1(s + 1)
-            quantize_x2(s + 1)
-            if live(s + 3):
-                widen(s + 3, both, True)
-            elif s + 1 < last and False:
-                empty_sim(s - 1, 0, nc.vector.tensor_copy)
-            empty_h(s, 0, nc.scalar.copy)
-            empty_h(s, 1, nc.scalar.copy)
-            if live(s - 1) and (live(s + 3) or not False) and s + 1 < last:
-                empty_sim(s - 1, 0, nc.scalar.copy)
-            if s + 1 < last:
-                quantize_h(s)
-        project(last)
-        empty_sim(last - 2, 0, nc.vector.tensor_copy)
-        quantize_h(last - 1)
-        compare(last - 1)
-        empty_sim(last - 2, 1, nc.scalar.copy)
-        empty_h(last, 0, nc.scalar.copy)
-        empty_h(last, 1, nc.vector.tensor_copy)
-        empty_sim(last - 1, 0, nc.scalar.copy)
-        quantize_h_block(last, 0)
-        quantize_h_block(last, 1)
-        compare(last)
-        empty_sim(last - 1, 1, nc.vector.tensor_copy)
-        empty_sim(last, 0, nc.scalar.copy)
-        empty_sim(last, 1, nc.vector.tensor_copy)
+        turn_x1(1)
+        turn_x2(1)
+        scale_x2(1)
+        empty_x1(1)
+        widen(3, (0, 1), False)
+        project(0)
+        quantize_x1(1)
+        quantize_x2(1)
+        empty_h(0, 0, nc.scalar.copy)
+        empty_h(0, 1, nc.scalar.copy)
+        quantize_h(0)
+        turn_x1(2)
+        turn_x2(2)
+        scale_x2(2)
+        empty_x1(2)
+        widen(4, (0, 1), False)
+        project(1)
+        compare(0, (0, 1))
+        quantize_x1(2)
+        quantize_x2(2)
+        empty_sim(0, 0, nc.vector.tensor_copy)
+        empty_h(1, 0, nc.scalar.copy)
+        empty_h(1, 1, nc.scalar.copy)
+        quantize_h(1)
+        turn_x1(3)
+        turn_x2(3)
+        empty_sim(0, 1, nc.scalar.copy)
+        scale_x2(3)
+        empty_x1(3)
+        project(2)
+        compare(1, (0, 1))
+        quantize_x1(3)
+        quantize_x2(3)
+        widen(5, (0, 1), True)
+        empty_h(2, 0, nc.scalar.copy)
+        empty_h(2, 1, nc.scalar.copy)
+        empty_sim(1, 0, nc.scalar.copy)
+        quantize_h(2)
+        turn_x1(4)
+        turn_x2(4)
+        empty_sim(1, 1, nc.scalar.copy)
+        scale_x2(4)
+        empty_x1(4)
+        project(3)
+        compare(2, (0, 1))
+        quantize_x1(4)
+        quantize_x2(4)
+        empty_h(3, 0, nc.scalar.copy)
+        empty_h(3, 1, nc.scalar.copy)
+        empty_sim(2, 0, nc.scalar.copy)
+        quantize_h(3)
+        turn_x1(5)
+        turn_x2(5)
+        scale_x2(5)
+        empty_x1(5)
+        empty_sim(2, 1, nc.scalar.copy)
+        project(4)
+        compare(3, (0, 1))
+        quantize_x1(5)
+        quantize_x2(5)
+        empty_h(4, 0, nc.scalar.copy)
+        empty_h(4, 1, nc.scalar.copy)
+        project(5)
+        empty_sim(3, 0, nc.vector.tensor_copy)
+        quantize_h(4)
+        compare(4, (0, 1))
+        empty_sim(3, 1, nc.scalar.copy)
+        empty_h(5, 0, nc.scalar.copy)
+        empty_h(5, 1, nc.vector.tensor_copy)
+        empty_sim(4, 0, nc.scalar.copy)
+        quantize_h_block(5, 0)
+        quantize_h_block(5, 1)
+        compare(5, (0, 1))
+        empty_sim(4, 1, nc.vector.tensor_copy)
+        empty_sim(5, 0, nc.scalar.copy)
+        empty_sim(5, 1, nc.vector.tensor_copy)

@@ -21,21 +21,33 @@ MULT = mybir.AluOpType.mult
 HALVES = 2 * B
 ROWS = 256
 BANKS = 8
-WIDE_ON_SCALAR = 4
+WIDE_ON_VECTOR = (0, 2)
+VECTOR_COPIES = {(8,2),(9,2),(10,2),(11,2),(9,1),(11,1),(13,1)}
 
 
 def tile_coattentionandcombine_pa_w4_kernel(tc, x1, w_words, w_scales, x2_bytes, x2_scale, out):
     nc = tc.nc
     with ExitStack() as ctx:
         keep = ctx.enter_context(tc.tile_pool(name="keep", bufs=1))
-        work = ctx.enter_context(tc.tile_pool(name="work", bufs=3))
-        psum = ctx.enter_context(tc.psum_pool(name="psum", bufs=2))
+        psum = ctx.enter_context(tc.psum_pool(name="psum", bufs=1))
         ctx.enter_context(tc.manual_schedule())
 
-        x1_raw = [keep.tile([P, 2 * D], BF16, name="x1_raw%d" % i) for i in range(HALVES)]
-        x2_raw = [keep.tile([P, 2 * D], U8, name="x2_raw%d" % i) for i in range(HALVES)]
+        def per_half(name, width, dtype):
+            return [keep.tile([P, width], dtype, name="%s%d" % (name, i), align_bytes=64) for i in range(HALVES)]
+
+        x1_raw = per_half("x1_raw", 2 * D, BF16)
+        x2_raw = per_half("x2_raw", 2 * D, U8)
+        x2_wide = per_half("x2_wide", 2 * D, BF16)
+        x1_k = per_half("x1_k", 4 * ROWS, BF16)
+        x2_k = per_half("x2_k", 4 * ROWS, BF16)
+        h_k = per_half("h_k", 4 * ROWS, BF16)
+        x1_words = per_half("x1_words", ROWS, U32)
+        x1_plane = per_half("x1_plane", ROWS, U8)
+        h_words = per_half("h_words", ROWS, U32)
+        h_plane = per_half("h_plane", ROWS, U8)
+        result = per_half("result", 2 * L, F32)
         x2_words = [keep.tile([P, L], U32, name="x2_words%d" % b, align_bytes=64) for b in range(B)]
-        x2_planes = [keep.tile([P, L], U8, name="x2_planes%d" % b, align_bytes=64) for b in range(B)]
+        x2_plane = [keep.tile([P, L], U8, name="x2_plane%d" % b, align_bytes=64) for b in range(B)]
         scale_col = keep.tile([P, 4], F32, name="scale_col")
         ones = keep.tile([P, 1], F32, name="ones")
         w_raw = keep.tile([P, 2 * D], U8, name="w_raw", align_bytes=64)
@@ -55,29 +67,28 @@ def tile_coattentionandcombine_pa_w4_kernel(tc, x1, w_words, w_scales, x2_bytes,
         def load_x2(i):
             nc.sync.dma_start(out=x2_raw[i][:], in_=x2_view[i // 2, i % 2])
 
-        nc.vector.memset(zeros[:], 0.0)
-        nc.vector.memset(w_raw_plane[:].bitcast(I32), 0)
-        nc.vector.memset(ones[:], 1.0)
-        nc.scalar.dma_start(out=scale_col[:], in_=x2_scale.rearrange("a o (p t) -> p (a o t)", t=4))
-        load_x1(0)
-        load_x2(0)
-        nc.sync.dma_start(out=w_raw[:].bitcast(I32), in_=w_words.rearrange("g p n -> p (g n)").bitcast(I32))
-        load_x2(1)
-        for q in range(4):
+        def load_scale():
+            nc.sync.dma_start(out=scale_col[:], in_=x2_scale.rearrange("a o (p t) -> p (a o t)", t=4))
+
+        def load_w():
+            nc.sync.dma_start(out=w_raw[:].bitcast(I32), in_=w_words.rearrange("g p n -> p (g n)").bitcast(I32))
+
+        def load_w_scales(q):
             nc.sync.dma_start(out=w_raw_plane[32 * q : 32 * q + 4, :].bitcast(I32), in_=w_scales[0, 4 * q : 4 * q + 4, :].bitcast(I32))
-        load_x1(1)
-        for i in range(2, HALVES):
-            load_x2(i)
-            load_x1(i)
-        make_identity(nc, ident[:])
 
-        wide, turned, k_first, x1_q, h_acc, h, h_q, sums = {}, {}, {}, {}, {}, {}, {}, {}
+        free_banks = list(range(BANKS))
+        held = {}
 
-        def quantize(rows, name):
-            words = work.tile([P, ROWS], U32, name=name + "_words", tag=name + "_words", align_bytes=64)
-            plane = work.tile([P, ROWS], U8, name=name + "_plane", tag=name + "_plane", align_bytes=64)
-            nc.vector.quantize_mx(out=words[:].bitcast(FP8X4), scales=plane[:], in_=rows[:])
-            return words, plane
+        def take_bank(key, shape):
+            bank = free_banks.pop(0)
+            acc = psum.tile(shape, F32, name="bank%d" % bank, tag="bank%d" % bank)
+            held[key] = bank, acc
+            return acc
+
+        def give_bank(key):
+            bank, acc = held.pop(key)
+            free_banks.append(bank)
+            return acc
 
         def order_w():
             nc.vector.tensor_copy(out=w[:].bitcast(U16).rearrange("p (t m) -> p t m", t=4), in_=w_raw[:].bitcast(U16).rearrange("p (m t) -> p t m", t=4))
@@ -85,251 +96,167 @@ def tile_coattentionandcombine_pa_w4_kernel(tc, x1, w_words, w_scales, x2_bytes,
         def order_w_plane():
             nc.vector.tensor_copy(out=w_plane[:].rearrange("p (t m) -> p t m", t=4), in_=w_raw_plane[:].rearrange("p (m t) -> p t m", t=4))
 
-        def widen(i, blocks, on_vector):
-            count = len(blocks)
-            rows = work.tile([P, count * D], BF16, name="x2_wide", tag="x2_wide", bufs=6)
-            codes = x2_raw[i][:, D * blocks[0] : D * (blocks[-1] + 1)].bitcast(E4M3)
-            words = rows[:].bitcast(F32)
-            if on_vector:
+        def widen(i):
+            codes = x2_raw[i][:].bitcast(E4M3)
+            if i in WIDE_ON_VECTOR:
                 nc.vector.tensor_scalar(
-                    out=rows[:].rearrange("p (u m e) -> p m u e", u=2, e=2),
+                    out=x2_wide[i][:].rearrange("p (u m e) -> p m u e", u=2, e=2),
                     in0=codes.rearrange("p (m u e) -> p m u e", u=2, e=2),
                     scalar1=ones[:],
                     scalar2=None,
                     op0=MULT,
                 )
             else:
-                nc.scalar.copy(out=rows[:], in_=codes)
-            for n, c in enumerate(blocks):
-                for u in range(2):
-                    if on_vector:
-                        wide[i, c, u] = words[:, P * (count * u + n) : P * (count * u + n + 1)]
-                    else:
-                        wide[i, c, u] = words[:, 256 * n + u : 256 * (n + 1) : 2]
+                nc.scalar.copy(out=x2_wide[i][:], in_=codes)
 
-        def turn(name, i, parts):
-            acc = psum.tile([P, 2, 2, P], F32, name=name + "_turned", tag="bank", bufs=BANKS)
+        def turn(name, i, words, split):
+            acc = take_bank((name, i), [P, 2, 2, P])
             for c in range(2):
                 for u in range(2):
-                    nc.tensor.transpose(acc[:, u, c, :], parts[c, u], ident[:])
-            turned[name, i] = acc
+                    part = words[:, P * (2 * u + c) : P * (2 * u + c + 1)] if split else words[:, 256 * c + u : 256 * (c + 1) : 2]
+                    nc.tensor.transpose(acc[:, u, c, :], part, ident[:])
 
         def turn_x1(i):
-            words = x1_raw[i][:].bitcast(F32)
-            turn("x1", i, dict(((c, u), words[:, 256 * c + u : 256 * (c + 1) : 2]) for c in range(2) for u in range(2)))
+            turn("x1", i, x1_raw[i][:].bitcast(F32), False)
 
         def turn_x2(i):
-            turn("x2", i, dict(((c, u), wide[i, c, u]) for c in range(2) for u in range(2)))
+            turn("x2", i, x2_wide[i][:].bitcast(F32), i in WIDE_ON_VECTOR)
 
         def empty_x1(i):
-            rows = work.tile([P, ROWS * 4], BF16, name="x1_k", tag="x1_k", align_bytes=64)
             nc.scalar.copy(
-                out=rows[:].bitcast(F32).rearrange("p (r u) -> p r u", u=2),
-                in_=turned["x1", i][:].rearrange("p u c r -> p (c r) u"),
+                out=x1_k[i][:].bitcast(F32).rearrange("p (r u) -> p r u", u=2),
+                in_=give_bank(("x1", i))[:].rearrange("p u c r -> p (c r) u"),
             )
-            k_first["x1", i] = rows
 
         def scale_x2(i):
-            rows = work.tile([P, ROWS * 4], BF16, name="x2_k", tag="x2_k", align_bytes=64)
             nc.vector.tensor_tensor(
-                out=rows[:].rearrange("p (r u e) -> p r u e", u=2, e=2),
-                in0=turned["x2", i][:].rearrange("p u c r -> p (u c r)").bitcast(BF16).rearrange("p (u r e) -> p r u e", u=2, e=2),
+                out=x2_k[i][:].rearrange("p (r u e) -> p r u e", u=2, e=2),
+                in0=give_bank(("x2", i))[:].rearrange("p u c r -> p (u c r)").bitcast(BF16).rearrange("p (u r e) -> p r u e", u=2, e=2),
                 in1=scale_col[:].rearrange("p (u e) -> p u e", u=2).unsqueeze(1).to_broadcast([P, ROWS, 2, 2]),
                 op=MULT,
             )
-            k_first["x2", i] = rows
 
         def quantize_x1(i):
-            x1_q[i] = quantize(k_first["x1", i], "x1")
+            nc.vector.quantize_mx(out=x1_words[i][:].bitcast(FP8X4), scales=x1_plane[i][:], in_=x1_k[i][:])
 
         def quantize_x2(i):
             b, j = divmod(i, 2)
             cols = slice(ROWS * j, ROWS * (j + 1))
-            nc.vector.quantize_mx(out=x2_words[b][:, cols].bitcast(FP8X4), scales=x2_planes[b][:, cols], in_=k_first["x2", i][:])
+            nc.vector.quantize_mx(out=x2_words[b][:, cols].bitcast(FP8X4), scales=x2_plane[b][:, cols], in_=x2_k[i][:])
 
-        def project(i):
-            words, plane = x1_q[i]
-            for c in range(2):
+        def project(i, blocks=(0, 1)):
+            for c in blocks:
                 rows = slice(P * c, P * (c + 1))
-                acc = psum.tile([P, 4, P], F32, name="h_acc", tag="bank", bufs=BANKS)
+                acc = take_bank(("h", i, c), [P, 4, P])
                 for t in range(4):
                     nc.tensor.matmul_mx(
                         out=acc[:, t, :],
                         lhsT=w[:, 256 * t : 256 * (t + 1)].bitcast(FP4X4),
                         lhsT_scale=w_plane[:, P * t : P * (t + 1)],
-                        rhs=words[:, rows].bitcast(FP8X4),
-                        rhs_scale=plane[:, rows],
+                        rhs=x1_words[i][:, rows].bitcast(FP8X4),
+                        rhs_scale=x1_plane[i][:, rows],
                         start=True,
                         stop=True,
                     )
-                h_acc[i, c] = acc
 
         def empty_h(i, c, copy):
-            if c == 0:
-                h_tile = work.tile([P, ROWS * 4], BF16, name="h", tag="h", align_bytes=64)
-                h[i] = h_tile
             copy(
-                out=h[i][:, 512 * c : 512 * (c + 1)].rearrange("p (r t) -> p r t", t=4),
-                in_=h_acc[i, c][:].rearrange("p t r -> p r t"),
+                out=h_k[i][:, 512 * c : 512 * (c + 1)].rearrange("p (r t) -> p r t", t=4),
+                in_=give_bank(("h", i, c))[:].rearrange("p t r -> p r t"),
             )
 
-        def quantize_h(i):
-            h_q[i] = quantize(h[i], "h")
+        def quantize_h(i, blocks=(0, 1)):
+            rows = slice(P * blocks[0], P * (blocks[-1] + 1))
+            nc.vector.quantize_mx(out=h_words[i][:, rows].bitcast(FP8X4), scales=h_plane[i][:, rows], in_=h_k[i][:, 4 * rows.start : 4 * rows.stop])
 
-        def quantize_h_block(i, c):
-            if c == 0:
-                words = work.tile([P, ROWS], U32, name="h_words", tag="h_words", align_bytes=64)
-                plane = work.tile([P, ROWS], U8, name="h_plane", tag="h_plane", align_bytes=64)
-                h_q[i] = words, plane
-            words, plane = h_q[i]
-            rows = slice(P * c, P * (c + 1))
-            nc.vector.quantize_mx(out=words[:, rows].bitcast(FP8X4), scales=plane[:, rows], in_=h[i][:, 512 * c : 512 * (c + 1)])
-
-        def compare(i, blocks=(0, 1), sides=(0, 1)):
+        def compare(i, blocks=(0, 1)):
             b = i // 2
-            words, plane = h_q[i]
-            cols = slice(ROWS * sides[0], ROWS * (sides[-1] + 1))
             for c in blocks:
                 rows = slice(P * c, P * (c + 1))
-                acc = psum.tile([P, ROWS * len(sides)], F32, name="sim_acc", tag="bank", bufs=BANKS)
                 nc.tensor.matmul_mx(
-                    out=acc[:],
-                    lhsT=words[:, rows].bitcast(FP8X4),
-                    lhsT_scale=plane[:, rows],
-                    rhs=x2_words[b][:, cols].bitcast(FP8X4),
-                    rhs_scale=x2_planes[b][:, cols],
+                    out=take_bank(("sim", i, c), [P, L])[:],
+                    lhsT=h_words[i][:, rows].bitcast(FP8X4),
+                    lhsT_scale=h_plane[i][:, rows],
+                    rhs=x2_words[b][:].bitcast(FP8X4),
+                    rhs_scale=x2_plane[b][:],
                     start=True,
                     stop=True,
                 )
-                sums[i, c, sides] = acc
 
-        def compare_side(i, side):
-            b = i // 2
-            words, plane = h_q[i]
-            cols = slice(ROWS * side, ROWS * (side + 1))
-            acc = psum.tile([P, 2, ROWS], F32, name="sim_acc", tag="bank", bufs=BANKS)
-            for c in range(2):
-                rows = slice(P * c, P * (c + 1))
-                nc.tensor.matmul_mx(
-                    out=acc[:, c, :],
-                    lhsT=words[:, rows].bitcast(FP8X4),
-                    lhsT_scale=plane[:, rows],
-                    rhs=x2_words[b][:, cols].bitcast(FP8X4),
-                    rhs_scale=x2_planes[b][:, cols],
-                    start=True,
-                    stop=True,
-                )
-            sums[i, side] = acc
-
-        def empty_side(i, side, copy):
+        def empty_sim(i, c, copy):
             b, j = divmod(i, 2)
-            result = work.tile([P, 2, ROWS], F32, name="result", tag="result", bufs=16)
-            copy(out=result[:].rearrange("p c (m e) -> p c m e", e=2), in_=sums[i, side][:].rearrange("p c (e m) -> p c m e", e=2))
-            nc.sync.dma_start(out=out_view[b, :, 2 * j : 2 * j + 2, ROWS * side : ROWS * (side + 1)], in_=result[:])
-
-        def empty_sim(i, c, copy, sides=(0, 1)):
-            b, j = divmod(i, 2)
-            cols = slice(ROWS * sides[0], ROWS * (sides[-1] + 1))
-            result = work.tile([P, ROWS * len(sides)], F32, name="result", tag="result", bufs=16)
-            copy(out=result[:].rearrange("p (s m e) -> p s m e", m=P, e=2), in_=sums[i, c, sides][:].rearrange("p (s e m) -> p s m e", m=P, e=2))
-            nc.sync.dma_start(out=out_view[b, :, 2 * j + c, cols], in_=result[:])
-
-        idle = psum.tile([P, P], F32, name="idle", tag="bank", bufs=BANKS)
+            rows = result[i][:, L * c : L * (c + 1)]
+            copy(out=rows.rearrange("p (s m e) -> p s m e", m=P, e=2), in_=give_bank(("sim", i, c))[:].rearrange("p (s e m) -> p s m e", m=P, e=2))
+            nc.sync.dma_start(out=out_view[b, :, 2 * j + c, :], in_=rows)
 
         def warm(count):
+            idle = take_bank("idle", [P, P])
             for k in range(count):
                 nc.tensor.matmul(out=idle[:], lhsT=zeros[:], rhs=zeros[:], start=True, stop=True)
+            give_bank("idle")
+
+        on_vector, on_scalar = nc.vector.tensor_copy, nc.scalar.copy
+
+        nc.vector.memset(zeros[:], 0.0)
+        nc.vector.memset(w_raw_plane[:].bitcast(I32), 0)
+        nc.vector.memset(ones[:], 1.0)
+        load_x2(0)
+        load_scale()
+        for i in range(1, 4):
+            load_x2(i)
+        load_w()
+        load_x1(0)
+        load_x2(4)
+        for q in range(4):
+            load_w_scales(q)
+        load_x1(1)
+        load_x2(5)
+        for i in range(2, HALVES):
+            load_x1(i)
+        make_identity(nc, ident[:])
 
         def live(i):
             return 0 <= i < HALVES
 
+        def copy_of(step, place):
+            return on_vector if (step, place) in VECTOR_COPIES else on_scalar
+
         warm(3)
-        turn_x1(0)
-        warm(1)
-        widen(0, (0, 1), True)
-        widen(1, (0, 1), False)
-        empty_x1(0)
-        order_w()
-        order_w_plane()
-        turn_x2(0)
-        warm(2)
-        widen(2, (0, 1), False)
-        scale_x2(0)
-        quantize_x1(0)
-        quantize_x2(0)
-        turn_x1(1)
-        turn_x2(1)
-        scale_x2(1)
-        empty_x1(1)
-        widen(3, (0, 1), False)
-        project(0)
-        quantize_x1(1)
-        quantize_x2(1)
-        empty_h(0, 0, nc.scalar.copy)
-        empty_h(0, 1, nc.scalar.copy)
-        quantize_h(0)
-        turn_x1(2)
-        turn_x2(2)
-        scale_x2(2)
-        empty_x1(2)
-        widen(4, (0, 1), False)
-        project(1)
-        compare(0, (0, 1))
-        quantize_x1(2)
-        quantize_x2(2)
-        empty_sim(0, 0, nc.vector.tensor_copy)
-        empty_h(1, 0, nc.scalar.copy)
-        empty_h(1, 1, nc.scalar.copy)
-        quantize_h(1)
-        turn_x1(3)
-        turn_x2(3)
-        empty_sim(0, 1, nc.scalar.copy)
-        scale_x2(3)
-        empty_x1(3)
-        project(2)
-        compare(1, (0, 1))
-        quantize_x1(3)
-        quantize_x2(3)
-        widen(5, (0, 1), True)
-        empty_h(2, 0, nc.scalar.copy)
-        empty_h(2, 1, nc.scalar.copy)
-        empty_sim(1, 0, nc.scalar.copy)
-        quantize_h(2)
-        turn_x1(4)
-        turn_x2(4)
-        empty_sim(1, 1, nc.scalar.copy)
-        scale_x2(4)
-        empty_x1(4)
-        project(3)
-        compare(2, (0, 1))
-        quantize_x1(4)
-        quantize_x2(4)
-        empty_h(3, 0, nc.scalar.copy)
-        empty_h(3, 1, nc.scalar.copy)
-        empty_sim(2, 0, nc.scalar.copy)
-        quantize_h(3)
-        turn_x1(5)
-        turn_x2(5)
-        scale_x2(5)
-        empty_x1(5)
-        empty_sim(2, 1, nc.scalar.copy)
-        project(4)
-        compare(3, (0, 1))
-        quantize_x1(5)
-        quantize_x2(5)
-        empty_h(4, 0, nc.scalar.copy)
-        empty_h(4, 1, nc.scalar.copy)
-        project(5)
-        empty_sim(3, 0, nc.vector.tensor_copy)
-        quantize_h(4)
-        compare(4, (0, 1))
-        empty_sim(3, 1, nc.scalar.copy)
-        empty_h(5, 0, nc.scalar.copy)
-        empty_h(5, 1, nc.vector.tensor_copy)
-        empty_sim(4, 0, nc.scalar.copy)
-        quantize_h_block(5, 0)
-        quantize_h_block(5, 1)
-        compare(5, (0, 1))
-        empty_sim(4, 1, nc.vector.tensor_copy)
-        empty_sim(5, 0, nc.scalar.copy)
-        empty_sim(5, 1, nc.vector.tensor_copy)
+        for s in range(-2, HALVES + 8):
+            if live(s - 6):
+                empty_h(s - 6, 0, copy_of(s, 0))
+            if s == 4:
+                order_w_plane()
+            if live(s - 4):
+                quantize_x1(s - 4)
+            if live(s - 2):
+                turn_x1(s - 2)
+            if live(s - 5):
+                project(s - 5)
+            if live(s + 1):
+                turn_x2(s + 1)
+            if s == -1:
+                warm(1)
+            if live(s - 8):
+                empty_sim(s - 8, 0, copy_of(s, 1))
+            if live(s - 6):
+                empty_h(s - 6, 1, copy_of(s, 2))
+            if live(s - 8):
+                empty_sim(s - 8, 1, copy_of(s, 3))
+            if live(s - 7):
+                compare(s - 7)
+            if live(s - 5):
+                quantize_x2(s - 5)
+            if s - 6 == HALVES - 1:
+                quantize_h(s - 6, (0,))
+                quantize_h(s - 6, (1,))
+            elif live(s - 6):
+                quantize_h(s - 6)
+            if live(s + 2):
+                widen(s + 2)
+            if s == 0:
+                order_w()
+            if live(s - 2):
+                empty_x1(s - 2)
+            if live(s - 1):
+                scale_x2(s - 1)

@@ -22,6 +22,7 @@ HALVES = 2 * B
 ROWS = 256
 BANKS = 8
 WIDE_ON_VECTOR = (0, 2)
+TURN_BY_MATMUL = (1, 3, 4, 5)
 VECTOR_COPIES = {(8,2),(9,2),(10,2),(11,2),(9,1),(11,1),(13,1)}
 
 
@@ -55,6 +56,7 @@ def tile_coattentionandcombine_pa_w4_kernel(tc, x1, w_words, w_scales, x2_bytes,
         w = keep.tile([P, 2 * D], U8, name="w", align_bytes=64)
         w_plane = keep.tile([P, D], U8, name="w_plane", align_bytes=64)
         ident = keep.tile([P, P], F32, name="ident")
+        ident_bf16 = keep.tile([P, P], BF16, name="ident_bf16")
         zeros = keep.tile([P, P], F32, name="zeros")
 
         x1_view = x1.rearrange("b (p j c) k -> b j p (c k)", j=2, c=2)
@@ -79,9 +81,9 @@ def tile_coattentionandcombine_pa_w4_kernel(tc, x1, w_words, w_scales, x2_bytes,
         free_banks = list(range(BANKS))
         held = {}
 
-        def take_bank(key, shape):
+        def take_bank(key, shape, dtype=F32):
             bank = free_banks.pop(0)
-            acc = psum.tile(shape, F32, name="bank%d" % bank, tag="bank%d" % bank)
+            acc = psum.tile(shape, dtype, name="bank%d" % bank, tag="bank%d" % bank)
             held[key] = bank, acc
             return acc
 
@@ -120,7 +122,13 @@ def tile_coattentionandcombine_pa_w4_kernel(tc, x1, w_words, w_scales, x2_bytes,
             turn("x1", i, x1_raw[i][:].bitcast(F32), False)
 
         def turn_x2(i):
-            turn("x2", i, x2_wide[i][:].bitcast(F32), i in WIDE_ON_VECTOR)
+            if i not in TURN_BY_MATMUL:
+                turn("x2", i, x2_wide[i][:].bitcast(F32), i in WIDE_ON_VECTOR)
+                return
+            acc = take_bank(("x2", i), [P, 4, ROWS], BF16)
+            for c in range(2):
+                for t in range(4):
+                    nc.tensor.matmul(out=acc[:, t, P * c : P * (c + 1)], lhsT=x2_wide[i][:, D * c + t : D * (c + 1) : 4], rhs=ident_bf16[:], start=True, stop=True)
 
         def empty_x1(i):
             nc.scalar.copy(
@@ -129,6 +137,14 @@ def tile_coattentionandcombine_pa_w4_kernel(tc, x1, w_words, w_scales, x2_bytes,
             )
 
         def scale_x2(i):
+            if i in TURN_BY_MATMUL:
+                nc.vector.tensor_tensor(
+                    out=x2_k[i][:].rearrange("p (r t) -> p r t", t=4),
+                    in0=give_bank(("x2", i))[:].rearrange("p t r -> p r t"),
+                    in1=scale_col[:].unsqueeze(1).to_broadcast([P, ROWS, 4]),
+                    op=MULT,
+                )
+                return
             nc.vector.tensor_tensor(
                 out=x2_k[i][:].rearrange("p (r u e) -> p r u e", u=2, e=2),
                 in0=give_bank(("x2", i))[:].rearrange("p u c r -> p (u c r)").bitcast(BF16).rearrange("p (u r e) -> p r u e", u=2, e=2),
@@ -214,6 +230,7 @@ def tile_coattentionandcombine_pa_w4_kernel(tc, x1, w_words, w_scales, x2_bytes,
         for i in range(2, HALVES):
             load_x1(i)
         make_identity(nc, ident[:])
+        nc.vector.tensor_copy(out=ident_bf16[:], in_=ident[:])
 
         def live(i):
             return 0 <= i < HALVES

@@ -21,9 +21,8 @@ MULT = mybir.AluOpType.mult
 HALVES = 2 * B
 ROWS = 256
 BANKS = 8
-WIDE_ON_VECTOR = (0, 2)
-TURN_BY_MATMUL = (1, 3, 4, 5)
-VECTOR_COPIES = {(8,2),(9,2),(10,2),(11,2),(9,1),(11,1),(13,1)}
+WIDE_ON_VECTOR = (0, 2,)
+TURN_BY_MATMUL = (1, 3, 5,)
 
 
 def tile_coattentionandcombine_pa_w4_kernel(tc, x1, w_words, w_scales, x2_bytes, x2_scale, out):
@@ -217,63 +216,73 @@ def tile_coattentionandcombine_pa_w4_kernel(tc, x1, w_words, w_scales, x2_bytes,
         nc.vector.memset(w_raw_plane[:].bitcast(I32), 0)
         nc.vector.memset(ones[:], 1.0)
         load_x2(0)
+        load_x2(1)
+        load_x2(2)
         load_scale()
-        for i in range(1, 4):
-            load_x2(i)
+        load_x2(3)
         load_w()
         load_x1(0)
-        load_x2(4)
-        for q in range(4):
-            load_w_scales(q)
         load_x1(1)
+        load_x2(4)
+        load_x1(2)
+        load_w_scales(0)
+        load_w_scales(1)
+        load_w_scales(2)
+        load_w_scales(3)
         load_x2(5)
-        for i in range(2, HALVES):
-            load_x1(i)
+        load_x1(3)
+        load_x1(4)
+        load_x1(5)
         make_identity(nc, ident[:])
         nc.vector.tensor_copy(out=ident_bf16[:], in_=ident[:])
 
-        def live(i):
-            return 0 <= i < HALVES
+        def empty_h_first(i):
+            empty_h(i, 0, on_vector if i in () else on_scalar)
 
-        def copy_of(step, place):
-            return on_vector if (step, place) in VECTOR_COPIES else on_scalar
+        def empty_h_second(i):
+            empty_h(i, 1, on_vector if i in () else on_scalar)
 
-        warm(3)
-        for s in range(-2, HALVES + 8):
-            if live(s - 6):
-                empty_h(s - 6, 0, copy_of(s, 0))
-            if s == 4:
-                order_w_plane()
-            if live(s - 4):
-                quantize_x1(s - 4)
-            if live(s - 2):
-                turn_x1(s - 2)
-            if live(s - 5):
-                project(s - 5)
-            if live(s + 1):
-                turn_x2(s + 1)
-            if s == -1:
-                warm(1)
-            if live(s - 8):
-                empty_sim(s - 8, 0, copy_of(s, 1))
-            if live(s - 6):
-                empty_h(s - 6, 1, copy_of(s, 2))
-            if live(s - 8):
-                empty_sim(s - 8, 1, copy_of(s, 3))
-            if live(s - 7):
-                compare(s - 7)
-            if live(s - 5):
-                quantize_x2(s - 5)
-            if s - 6 == HALVES - 1:
-                quantize_h(s - 6, (0,))
-                quantize_h(s - 6, (1,))
-            elif live(s - 6):
-                quantize_h(s - 6)
-            if live(s + 2):
-                widen(s + 2)
-            if s == 0:
+        def empty_sim_first(i):
+            empty_sim(i, 0, on_vector if i in () else on_scalar)
+
+        def empty_sim_second(i):
+            empty_sim(i, 1, on_vector if i in (1, 2, 3, 4, 5,) else on_scalar)
+
+        def quantize_h_half(i):
+            if i == HALVES - 1:
+                quantize_h(i, (0,))
+                quantize_h(i, (1,))
+            else:
+                quantize_h(i)
+
+        def order_w_once(i):
+            if i == 0:
                 order_w()
-            if live(s - 2):
-                empty_x1(s - 2)
-            if live(s - 1):
-                scale_x2(s - 1)
+
+        def order_w_plane_once(i):
+            if i == 0:
+                order_w_plane()
+
+        stages = [
+            (turn_x1, 5),
+            (quantize_h_half, 10),
+            (empty_sim_first, 11),
+            (compare, 10),
+            (empty_h_first, 9),
+            (order_w_plane_once, 8),
+            (quantize_x1, 8),
+            (empty_h_second, 9),
+            (empty_sim_second, 11),
+            (project, 8),
+            (scale_x2, 6),
+            (turn_x2, 3),
+            (empty_x1, 5),
+            (quantize_x2, 8),
+            (widen, 0),
+            (order_w_once, 5),
+        ]
+        warm(4)
+        for step in range(HALVES + max(lag for stage, lag in stages)):
+            for stage, lag in stages:
+                if 0 <= step - lag < HALVES:
+                    stage(step - lag)

@@ -21,7 +21,7 @@ MULT = mybir.AluOpType.mult
 HALVES = 2 * B
 ROWS = 256
 BANKS = 8
-WIDE_ON_VECTOR = (0, 2,)
+WIDE_ON_VECTOR = (0,)
 TURN_BY_MATMUL = (1, 3, 5,)
 
 
@@ -217,36 +217,35 @@ def tile_coattentionandcombine_pa_w4_kernel(tc, x1, w_words, w_scales, x2_bytes,
         nc.vector.memset(ones[:], 1.0)
         load_x2(0)
         load_x2(1)
-        load_x2(2)
         load_scale()
-        load_x2(3)
+        load_x2(2)
         load_w()
         load_x1(0)
+        load_x2(3)
         load_x1(1)
-        load_x2(4)
-        load_x1(2)
         load_w_scales(0)
         load_w_scales(1)
         load_w_scales(2)
         load_w_scales(3)
+        load_x2(4)
+        load_x1(2)
         load_x2(5)
         load_x1(3)
         load_x1(4)
         load_x1(5)
         make_identity(nc, ident[:])
-        nc.vector.tensor_copy(out=ident_bf16[:], in_=ident[:])
 
         def empty_h_first(i):
-            empty_h(i, 0, on_vector if i in () else on_scalar)
+            empty_h(i, 0, on_vector if i in (5,) else on_scalar)
 
         def empty_h_second(i):
-            empty_h(i, 1, on_vector if i in () else on_scalar)
+            empty_h(i, 1, on_vector if i in (2, 3, 4, 5,) else on_scalar)
 
         def empty_sim_first(i):
             empty_sim(i, 0, on_vector if i in () else on_scalar)
 
         def empty_sim_second(i):
-            empty_sim(i, 1, on_vector if i in (1, 2, 3, 4, 5,) else on_scalar)
+            empty_sim(i, 1, on_vector if i in (5,) else on_scalar)
 
         def quantize_h_half(i):
             if i == HALVES - 1:
@@ -257,6 +256,7 @@ def tile_coattentionandcombine_pa_w4_kernel(tc, x1, w_words, w_scales, x2_bytes,
 
         def order_w_once(i):
             if i == 0:
+                nc.vector.tensor_copy(out=ident_bf16[:], in_=ident[:])
                 order_w()
 
         def order_w_plane_once(i):
@@ -264,24 +264,24 @@ def tile_coattentionandcombine_pa_w4_kernel(tc, x1, w_words, w_scales, x2_bytes,
                 order_w_plane()
 
         stages = [
-            (turn_x1, 5),
-            (quantize_h_half, 10),
-            (empty_sim_first, 11),
-            (compare, 10),
-            (empty_h_first, 9),
-            (order_w_plane_once, 8),
-            (quantize_x1, 8),
-            (empty_h_second, 9),
-            (empty_sim_second, 11),
-            (project, 8),
-            (scale_x2, 6),
-            (turn_x2, 3),
-            (empty_x1, 5),
-            (quantize_x2, 8),
+            (turn_x2, 2),
+            (scale_x2, 3),
+            (empty_sim_first, 8),
+            (quantize_x1, 4),
+            (order_w_plane_once, 4),
+            (turn_x1, 3),
+            (empty_h_second, 6),
+            (project, 5),
+            (quantize_x2, 5),
+            (empty_sim_second, 8),
             (widen, 0),
-            (order_w_once, 5),
+            (order_w_once, 1),
+            (empty_x1, 3),
+            (compare, 7),
+            (quantize_h_half, 6),
+            (empty_h_first, 5),
         ]
-        warm(4)
+        warm(3)
         for step in range(HALVES + max(lag for stage, lag in stages)):
             for stage, lag in stages:
                 if 0 <= step - lag < HALVES:

@@ -139,15 +139,15 @@ def tile_coattentionandcombine_pa_w4_kernel(tc, x1, w_words, w_scales, x2_bytes,
             if i in TURN_BY_MATMUL:
                 nc.vector.tensor_tensor(
                     out=x2_k[i][:].rearrange("p (r t) -> p r t", t=4),
-                    in0=give_bank(("x2", i))[:].rearrange("p t r -> p r t"),
-                    in1=scale_col[:].unsqueeze(1).to_broadcast([P, ROWS, 4]),
+                    in1=give_bank(("x2", i))[:].rearrange("p t r -> p r t"),
+                    in0=scale_col[:].unsqueeze(1).to_broadcast([P, ROWS, 4]),
                     op=MULT,
                 )
                 return
             nc.vector.tensor_tensor(
                 out=x2_k[i][:].rearrange("p (r u e) -> p r u e", u=2, e=2),
-                in0=give_bank(("x2", i))[:].rearrange("p u c r -> p (u c r)").bitcast(BF16).rearrange("p (u r e) -> p r u e", u=2, e=2),
-                in1=scale_col[:].rearrange("p (u e) -> p u e", u=2).unsqueeze(1).to_broadcast([P, ROWS, 2, 2]),
+                in1=give_bank(("x2", i))[:].rearrange("p u c r -> p (u c r)").bitcast(BF16).rearrange("p (u r e) -> p r u e", u=2, e=2),
+                in0=scale_col[:].rearrange("p (u e) -> p u e", u=2).unsqueeze(1).to_broadcast([P, ROWS, 2, 2]),
                 op=MULT,
             )
 

@@ -19,10 +19,12 @@ FP4X4 = mybir.dt.float4_e2m1fn_x4
 MULT = mybir.AluOpType.mult
 
 HALVES = 2 * B
+LAST = HALVES - 1
 ROWS = 256
 BANKS = 8
-WIDE_ON_VECTOR = (0,)
-TURN_BY_MATMUL = (1, 3, 5,)
+WARM_UPS = 3
+WIDEN_AHEAD = 2
+H_ON_VECTOR_FROM = 7
 
 
 def tile_coattentionandcombine_pa_w4_kernel(tc, x1, w_words, w_scales, x2_bytes, x2_scale, out):
@@ -68,15 +70,6 @@ def tile_coattentionandcombine_pa_w4_kernel(tc, x1, w_words, w_scales, x2_bytes,
         def load_x2(i):
             nc.sync.dma_start(out=x2_raw[i][:], in_=x2_view[i // 2, i % 2])
 
-        def load_scale():
-            nc.sync.dma_start(out=scale_col[:], in_=x2_scale.rearrange("a o (p t) -> p (a o t)", t=4))
-
-        def load_w():
-            nc.sync.dma_start(out=w_raw[:].bitcast(I32), in_=w_words.rearrange("g p n -> p (g n)").bitcast(I32))
-
-        def load_w_scales(q):
-            nc.sync.dma_start(out=w_raw_plane[32 * q : 32 * q + 4, :].bitcast(I32), in_=w_scales[0, 4 * q : 4 * q + 4, :].bitcast(I32))
-
         free_banks = list(range(BANKS))
         held = {}
 
@@ -91,15 +84,9 @@ def tile_coattentionandcombine_pa_w4_kernel(tc, x1, w_words, w_scales, x2_bytes,
             free_banks.append(bank)
             return acc
 
-        def order_w():
-            nc.vector.tensor_copy(out=w[:].bitcast(U16).rearrange("p (t m) -> p t m", t=4), in_=w_raw[:].bitcast(U16).rearrange("p (m t) -> p t m", t=4))
-
-        def order_w_plane():
-            nc.vector.tensor_copy(out=w_plane[:].rearrange("p (t m) -> p t m", t=4), in_=w_raw_plane[:].rearrange("p (m t) -> p t m", t=4))
-
         def widen(i):
             codes = x2_raw[i][:].bitcast(E4M3)
-            if i in WIDE_ON_VECTOR:
+            if i == 0:
                 nc.vector.tensor_scalar(
                     out=x2_wide[i][:].rearrange("p (u m e) -> p m u e", u=2, e=2),
                     in0=codes.rearrange("p (m u e) -> p m u e", u=2, e=2),
@@ -110,24 +97,38 @@ def tile_coattentionandcombine_pa_w4_kernel(tc, x1, w_words, w_scales, x2_bytes,
             else:
                 nc.scalar.copy(out=x2_wide[i][:], in_=codes)
 
-        def turn(name, i, words, split):
-            acc = take_bank((name, i), [P, 2, 2, P])
+        def turn_pairs(key, part):
+            acc = take_bank(key, [P, 2, 2, P])
             for c in range(2):
                 for u in range(2):
-                    part = words[:, P * (2 * u + c) : P * (2 * u + c + 1)] if split else words[:, 256 * c + u : 256 * (c + 1) : 2]
-                    nc.tensor.transpose(acc[:, u, c, :], part, ident[:])
+                    nc.tensor.transpose(acc[:, u, c, :], part(c, u), ident[:])
+
+        def every_second(pairs):
+            return lambda c, u: pairs[:, 256 * c + u : 256 * (c + 1) : 2]
 
         def turn_x1(i):
-            turn("x1", i, x1_raw[i][:].bitcast(F32), False)
+            turn_pairs(("x1", i), every_second(x1_raw[i][:].bitcast(F32)))
 
         def turn_x2(i):
-            if i not in TURN_BY_MATMUL:
-                turn("x2", i, x2_wide[i][:].bitcast(F32), i in WIDE_ON_VECTOR)
-                return
-            acc = take_bank(("x2", i), [P, 4, ROWS], BF16)
-            for c in range(2):
-                for t in range(4):
-                    nc.tensor.matmul(out=acc[:, t, P * c : P * (c + 1)], lhsT=x2_wide[i][:, D * c + t : D * (c + 1) : 4], rhs=ident_bf16[:], start=True, stop=True)
+            pairs = x2_wide[i][:].bitcast(F32)
+            if i == 0:
+                turn_pairs(("x2", i), lambda c, u: pairs[:, P * (2 * u + c) : P * (2 * u + c + 1)])
+            elif by_matmul(i):
+                acc = take_bank(("x2", i), [P, 4, ROWS], BF16)
+                for c in range(2):
+                    for t in range(4):
+                        nc.tensor.matmul(
+                            out=acc[:, t, P * c : P * (c + 1)],
+                            lhsT=x2_wide[i][:, D * c + t : D * (c + 1) : 4],
+                            rhs=ident_bf16[:],
+                            start=True,
+                            stop=True,
+                        )
+            else:
+                turn_pairs(("x2", i), every_second(pairs))
+
+        def by_matmul(i):
+            return i % 2 == 1
 
         def empty_x1(i):
             nc.scalar.copy(
@@ -136,20 +137,21 @@ def tile_coattentionandcombine_pa_w4_kernel(tc, x1, w_words, w_scales, x2_bytes,
             )
 
         def scale_x2(i):
-            if i in TURN_BY_MATMUL:
+            acc = give_bank(("x2", i))
+            if by_matmul(i):
                 nc.vector.tensor_tensor(
                     out=x2_k[i][:].rearrange("p (r t) -> p r t", t=4),
-                    in1=give_bank(("x2", i))[:].rearrange("p t r -> p r t"),
                     in0=scale_col[:].unsqueeze(1).to_broadcast([P, ROWS, 4]),
+                    in1=acc[:].rearrange("p t r -> p r t"),
                     op=MULT,
                 )
-                return
-            nc.vector.tensor_tensor(
-                out=x2_k[i][:].rearrange("p (r u e) -> p r u e", u=2, e=2),
-                in1=give_bank(("x2", i))[:].rearrange("p u c r -> p (u c r)").bitcast(BF16).rearrange("p (u r e) -> p r u e", u=2, e=2),
-                in0=scale_col[:].rearrange("p (u e) -> p u e", u=2).unsqueeze(1).to_broadcast([P, ROWS, 2, 2]),
-                op=MULT,
-            )
+            else:
+                nc.vector.tensor_tensor(
+                    out=x2_k[i][:].rearrange("p (r u e) -> p r u e", u=2, e=2),
+                    in0=scale_col[:].rearrange("p (u e) -> p u e", u=2).unsqueeze(1).to_broadcast([P, ROWS, 2, 2]),
+                    in1=acc[:].rearrange("p u c r -> p (u c r)").bitcast(BF16).rearrange("p (u r e) -> p r u e", u=2, e=2),
+                    op=MULT,
+                )
 
         def quantize_x1(i):
             nc.vector.quantize_mx(out=x1_words[i][:].bitcast(FP8X4), scales=x1_plane[i][:], in_=x1_k[i][:])
@@ -159,8 +161,17 @@ def tile_coattentionandcombine_pa_w4_kernel(tc, x1, w_words, w_scales, x2_bytes,
             cols = slice(ROWS * j, ROWS * (j + 1))
             nc.vector.quantize_mx(out=x2_words[b][:, cols].bitcast(FP8X4), scales=x2_plane[b][:, cols], in_=x2_k[i][:])
 
-        def project(i, blocks=(0, 1)):
-            for c in blocks:
+        def quantize_h(i):
+            for first, count in ((0, P), (P, P)) if i == LAST else ((0, ROWS),):
+                rows = slice(first, first + count)
+                nc.vector.quantize_mx(
+                    out=h_words[i][:, rows].bitcast(FP8X4),
+                    scales=h_plane[i][:, rows],
+                    in_=h_k[i][:, 4 * first : 4 * (first + count)],
+                )
+
+        def project(i):
+            for c in range(2):
                 rows = slice(P * c, P * (c + 1))
                 acc = take_bank(("h", i, c), [P, 4, P])
                 for t in range(4):
@@ -174,19 +185,16 @@ def tile_coattentionandcombine_pa_w4_kernel(tc, x1, w_words, w_scales, x2_bytes,
                         stop=True,
                     )
 
-        def empty_h(i, c, copy):
+        def empty_h(i, c):
+            copy = nc.vector.tensor_copy if 2 * i + c >= H_ON_VECTOR_FROM else nc.scalar.copy
             copy(
                 out=h_k[i][:, 512 * c : 512 * (c + 1)].rearrange("p (r t) -> p r t", t=4),
                 in_=give_bank(("h", i, c))[:].rearrange("p t r -> p r t"),
             )
 
-        def quantize_h(i, blocks=(0, 1)):
-            rows = slice(P * blocks[0], P * (blocks[-1] + 1))
-            nc.vector.quantize_mx(out=h_words[i][:, rows].bitcast(FP8X4), scales=h_plane[i][:, rows], in_=h_k[i][:, 4 * rows.start : 4 * rows.stop])
-
-        def compare(i, blocks=(0, 1)):
+        def compare(i):
             b = i // 2
-            for c in blocks:
+            for c in range(2):
                 rows = slice(P * c, P * (c + 1))
                 nc.tensor.matmul_mx(
                     out=take_bank(("sim", i, c), [P, L])[:],
@@ -198,91 +206,71 @@ def tile_coattentionandcombine_pa_w4_kernel(tc, x1, w_words, w_scales, x2_bytes,
                     stop=True,
                 )
 
-        def empty_sim(i, c, copy):
+        def empty_sim(i, c):
             b, j = divmod(i, 2)
+            copy = nc.vector.tensor_copy if (i, c) == (LAST, 1) else nc.scalar.copy
             rows = result[i][:, L * c : L * (c + 1)]
-            copy(out=rows.rearrange("p (s m e) -> p s m e", m=P, e=2), in_=give_bank(("sim", i, c))[:].rearrange("p (s e m) -> p s m e", m=P, e=2))
+            copy(
+                out=rows.rearrange("p (s m e) -> p s m e", m=P, e=2),
+                in_=give_bank(("sim", i, c))[:].rearrange("p (s e m) -> p s m e", m=P, e=2),
+            )
             nc.sync.dma_start(out=out_view[b, :, 2 * j + c, :], in_=rows)
-
-        def warm(count):
-            idle = take_bank("idle", [P, P])
-            for k in range(count):
-                nc.tensor.matmul(out=idle[:], lhsT=zeros[:], rhs=zeros[:], start=True, stop=True)
-            give_bank("idle")
-
-        on_vector, on_scalar = nc.vector.tensor_copy, nc.scalar.copy
 
         nc.vector.memset(zeros[:], 0.0)
         nc.vector.memset(w_raw_plane[:].bitcast(I32), 0)
         nc.vector.memset(ones[:], 1.0)
+
         load_x2(0)
         load_x2(1)
-        load_scale()
+        nc.sync.dma_start(out=scale_col[:], in_=x2_scale.rearrange("a o (p t) -> p (a o t)", t=4))
         load_x2(2)
-        load_w()
-        load_x1(0)
-        load_x2(3)
-        load_x1(1)
-        load_w_scales(0)
-        load_w_scales(1)
-        load_w_scales(2)
-        load_w_scales(3)
-        load_x2(4)
-        load_x1(2)
-        load_x2(5)
-        load_x1(3)
-        load_x1(4)
-        load_x1(5)
+        nc.sync.dma_start(out=w_raw[:].bitcast(I32), in_=w_words.rearrange("g p n -> p (g n)").bitcast(I32))
+        for i in range(HALVES):
+            load_x1(i)
+            if i == 1:
+                for q in range(4):
+                    nc.sync.dma_start(
+                        out=w_raw_plane[32 * q : 32 * q + 4, :].bitcast(I32),
+                        in_=w_scales[0, 4 * q : 4 * q + 4, :].bitcast(I32),
+                    )
+            if i + 3 < HALVES:
+                load_x2(i + 3)
+
         make_identity(nc, ident[:])
 
-        def empty_h_first(i):
-            empty_h(i, 0, on_vector if i in (5,) else on_scalar)
+        idle = take_bank("idle", [P, P])
+        for k in range(WARM_UPS):
+            nc.tensor.matmul(out=idle[:], lhsT=zeros[:], rhs=zeros[:], start=True, stop=True)
+        give_bank("idle")
 
-        def empty_h_second(i):
-            empty_h(i, 1, on_vector if i in (2, 3, 4, 5,) else on_scalar)
+        def at(stage, i, *more):
+            if 0 <= i < HALVES:
+                stage(i, *more)
 
-        def empty_sim_first(i):
-            empty_sim(i, 0, on_vector if i in () else on_scalar)
+        for s in range(-1 - WIDEN_AHEAD, HALVES + 5):
+            at(empty_sim, s - 5, 0)
+            at(empty_h, s - 3, 1)
+            at(empty_sim, s - 5, 1)
 
-        def empty_sim_second(i):
-            empty_sim(i, 1, on_vector if i in (5,) else on_scalar)
+            at(turn_x2, s + 1)
+            at(turn_x1, s)
 
-        def quantize_h_half(i):
-            if i == HALVES - 1:
-                quantize_h(i, (0,))
-                quantize_h(i, (1,))
-            else:
-                quantize_h(i)
+            at(scale_x2, s)
+            at(quantize_x1, s - 1)
+            if s == 1:
+                nc.vector.tensor_copy(out=w_plane[:].rearrange("p (t m) -> p t m", t=4), in_=w_raw_plane[:].rearrange("p (m t) -> p t m", t=4))
+            at(quantize_x2, s - 2)
+            at(quantize_h, s - 3)
 
-        def order_w_once(i):
-            if i == 0:
+            at(project, s - 2)
+            at(compare, s - 4)
+
+            at(widen, s + 1 + WIDEN_AHEAD)
+            if s == -1 - WIDEN_AHEAD:
                 nc.vector.tensor_copy(out=ident_bf16[:], in_=ident[:])
-                order_w()
-
-        def order_w_plane_once(i):
-            if i == 0:
-                order_w_plane()
-
-        stages = [
-            (turn_x2, 2),
-            (scale_x2, 3),
-            (empty_sim_first, 8),
-            (quantize_x1, 4),
-            (order_w_plane_once, 4),
-            (turn_x1, 3),
-            (empty_h_second, 6),
-            (project, 5),
-            (quantize_x2, 5),
-            (empty_sim_second, 8),
-            (widen, 0),
-            (order_w_once, 1),
-            (empty_x1, 3),
-            (compare, 7),
-            (quantize_h_half, 6),
-            (empty_h_first, 5),
-        ]
-        warm(3)
-        for step in range(HALVES + max(lag for stage, lag in stages)):
-            for stage, lag in stages:
-                if 0 <= step - lag < HALVES:
-                    stage(step - lag)
+                nc.vector.tensor_copy(
+                    out=w[:].bitcast(U16).rearrange("p (t m) -> p t m", t=4),
+                    in_=w_raw[:].bitcast(U16).rearrange("p (m t) -> p t m", t=4),
+                )
+            at(empty_x1, s)
+            at(empty_h, s - 2, 0)

@@ -24,7 +24,7 @@ ROWS = 256
 BANKS = 8
 WARM_UPS = 3
 WIDEN_AHEAD = 2
-H_ON_VECTOR_FROM = 7
+H_ON_VECTOR_FROM = 2
 
 
 def tile_coattentionandcombine_pa_w4_kernel(tc, x1, w_words, w_scales, x2_bytes, x2_scale, out):
@@ -186,7 +186,7 @@ def tile_coattentionandcombine_pa_w4_kernel(tc, x1, w_words, w_scales, x2_bytes,
                     )
 
         def empty_h(i, c):
-            copy = nc.vector.tensor_copy if 2 * i + c >= H_ON_VECTOR_FROM else nc.scalar.copy
+            copy = nc.vector.tensor_copy if (c == 1 and i >= H_ON_VECTOR_FROM) or i == LAST else nc.scalar.copy
             copy(
                 out=h_k[i][:, 512 * c : 512 * (c + 1)].rearrange("p (r t) -> p r t", t=4),
                 in_=give_bank(("h", i, c))[:].rearrange("p t r -> p r t"),
@@ -221,8 +221,8 @@ def tile_coattentionandcombine_pa_w4_kernel(tc, x1, w_words, w_scales, x2_bytes,
         nc.vector.memset(ones[:], 1.0)
 
         load_x2(0)
-        load_x2(1)
         nc.sync.dma_start(out=scale_col[:], in_=x2_scale.rearrange("a o (p t) -> p (a o t)", t=4))
+        load_x2(1)
         load_x2(2)
         nc.sync.dma_start(out=w_raw[:].bitcast(I32), in_=w_words.rearrange("g p n -> p (g n)").bitcast(I32))
         for i in range(HALVES):
@@ -249,8 +249,6 @@ def tile_coattentionandcombine_pa_w4_kernel(tc, x1, w_words, w_scales, x2_bytes,
 
         for s in range(-1 - WIDEN_AHEAD, HALVES + 5):
             at(empty_sim, s - 5, 0)
-            at(empty_h, s - 3, 1)
-            at(empty_sim, s - 5, 1)
 
             at(turn_x2, s + 1)
             at(turn_x1, s)
@@ -259,7 +257,9 @@ def tile_coattentionandcombine_pa_w4_kernel(tc, x1, w_words, w_scales, x2_bytes,
             at(quantize_x1, s - 1)
             if s == 1:
                 nc.vector.tensor_copy(out=w_plane[:].rearrange("p (t m) -> p t m", t=4), in_=w_raw_plane[:].rearrange("p (m t) -> p t m", t=4))
+            at(empty_h, s - 3, 1)
             at(quantize_x2, s - 2)
+            at(empty_sim, s - 5, 1)
             at(quantize_h, s - 3)
 
             at(project, s - 2)

@@ -22,7 +22,7 @@ HALVES = 2 * B
 LAST = HALVES - 1
 ROWS = 256
 BANKS = 8
-WARM_UPS = 3
+WARM_UPS = 4
 WIDEN_AHEAD = 2
 H_ON_VECTOR_FROM = 2
 

@@ -23,8 +23,7 @@ LAST = HALVES - 1
 ROWS = 256
 BANKS = 8
 WARM_UPS = 4
-WIDEN_AHEAD = 2
-H_ON_VECTOR_FROM = 2
+BY_MATMUL = (1, 3, 5)
 
 
 def tile_coattentionandcombine_pa_w4_kernel(tc, x1, w_words, w_scales, x2_bytes, x2_scale, out):
@@ -34,31 +33,35 @@ def tile_coattentionandcombine_pa_w4_kernel(tc, x1, w_words, w_scales, x2_bytes,
         psum = ctx.enter_context(tc.psum_pool(name="psum", bufs=1))
         ctx.enter_context(tc.manual_schedule())
 
+        def sbuf(name, width, dtype, tag=None):
+            return keep.tile([P, width], dtype, name=name, tag=tag or name, align_bytes=64)
+
         def per_half(name, width, dtype):
-            return [keep.tile([P, width], dtype, name="%s%d" % (name, i), align_bytes=64) for i in range(HALVES)]
+            return [sbuf("%s%d" % (name, i), width, dtype) for i in range(HALVES)]
 
         x1_raw = per_half("x1_raw", 2 * D, BF16)
         x2_raw = per_half("x2_raw", 2 * D, U8)
-        x2_wide = per_half("x2_wide", 2 * D, BF16)
         x1_k = per_half("x1_k", 4 * ROWS, BF16)
-        x2_k = per_half("x2_k", 4 * ROWS, BF16)
         h_k = per_half("h_k", 4 * ROWS, BF16)
         x1_words = per_half("x1_words", ROWS, U32)
         x1_plane = per_half("x1_plane", ROWS, U8)
         h_words = per_half("h_words", ROWS, U32)
         h_plane = per_half("h_plane", ROWS, U8)
         result = per_half("result", 2 * L, F32)
-        x2_words = [keep.tile([P, L], U32, name="x2_words%d" % b, align_bytes=64) for b in range(B)]
-        x2_plane = [keep.tile([P, L], U8, name="x2_plane%d" % b, align_bytes=64) for b in range(B)]
-        scale_col = keep.tile([P, 4], F32, name="scale_col")
-        ones = keep.tile([P, 1], F32, name="ones")
-        w_raw = keep.tile([P, 2 * D], U8, name="w_raw", align_bytes=64)
-        w_raw_plane = keep.tile([P, D], U8, name="w_raw_plane", align_bytes=64)
-        w = keep.tile([P, 2 * D], U8, name="w", align_bytes=64)
-        w_plane = keep.tile([P, D], U8, name="w_plane", align_bytes=64)
-        ident = keep.tile([P, P], F32, name="ident")
-        ident_bf16 = keep.tile([P, P], BF16, name="ident_bf16")
-        zeros = keep.tile([P, P], F32, name="zeros")
+        x2_words = [sbuf("x2_words%d" % b, L, U32) for b in range(B)]
+        x2_plane = [sbuf("x2_plane%d" % b, L, U8) for b in range(B)]
+        x2_wide = {}
+        x2_k_batch = [sbuf("x2_k%d" % b, 4 * L, BF16) for b in range(B)]
+        x2_k = [x2_k_batch[i // 2][:, 4 * ROWS * (i % 2) : 4 * ROWS * (i % 2 + 1)] for i in range(HALVES)]
+        scale_col = sbuf("scale_col", 16, F32)
+        w_raw = sbuf("w_raw", 2 * D, U8)
+        w_raw_plane = sbuf("w_raw_plane", D, U8)
+        w_rows = keep.tile([4, 4, D // 4], I32, name="w_rows")
+        w = sbuf("w", 2 * D, U8)
+        w_plane = sbuf("w_plane", D, U8)
+        ident = sbuf("ident", P, F32)
+        ident_bf16 = sbuf("ident_bf16", P, BF16)
+        zeros = sbuf("zeros", P, F32)
 
         x1_view = x1.rearrange("b (p j c) k -> b j p (c k)", j=2, c=2)
         x2_view = x2_bytes.rearrange("b (j p c) k -> b j p (c k)", j=2, c=2)
@@ -69,6 +72,21 @@ def tile_coattentionandcombine_pa_w4_kernel(tc, x1, w_words, w_scales, x2_bytes,
 
         def load_x2(i):
             nc.sync.dma_start(out=x2_raw[i][:], in_=x2_view[i // 2, i % 2])
+
+        def load_scale_col():
+            by_run = x2_scale.rearrange("a o (q u j e) -> (a o u) q j e", u=2, j=8, e=2)
+            for u in range(2):
+                nc.sync.dma_start(out=scale_col[:, 8 * u : 8 * u + 2], in_=by_run[u])
+
+        def load_w():
+            nc.sync.dma_start(out=w_raw[:].bitcast(I32), in_=w_words.rearrange("g p n -> p (g n)").bitcast(I32))
+
+        def load_w_plane():
+            nc.sync.dma_start(out=w_rows[:], in_=w_scales.bitcast(I32).rearrange("g (q r) n -> r (g q) n", r=4))
+
+        def spread_w_plane():
+            for q in range(4):
+                nc.vector.tensor_copy(out=w_raw_plane[32 * q : 32 * q + 4, :].bitcast(I32), in_=w_rows[:, q, :])
 
         free_banks = list(range(BANKS))
         held = {}
@@ -84,18 +102,12 @@ def tile_coattentionandcombine_pa_w4_kernel(tc, x1, w_words, w_scales, x2_bytes,
             free_banks.append(bank)
             return acc
 
-        def widen(i):
-            codes = x2_raw[i][:].bitcast(E4M3)
-            if i == 0:
-                nc.vector.tensor_scalar(
-                    out=x2_wide[i][:].rearrange("p (u m e) -> p m u e", u=2, e=2),
-                    in0=codes.rearrange("p (m u e) -> p m u e", u=2, e=2),
-                    scalar1=ones[:],
-                    scalar2=None,
-                    op0=MULT,
-                )
-            else:
-                nc.scalar.copy(out=x2_wide[i][:], in_=codes)
+        def widen(i, copy, tag):
+            x2_wide[i] = sbuf("x2_wide%d" % i, 2 * D, BF16, tag)
+            copy(
+                out=x2_wide[i][:].rearrange("p (u q k) -> p q u k", u=2, k=16),
+                in_=x2_raw[i][:].bitcast(E4M3).rearrange("p (q u k) -> p q u k", u=2, k=16),
+            )
 
         def turn_pairs(key, part):
             acc = take_bank(key, [P, 2, 2, P])
@@ -103,55 +115,51 @@ def tile_coattentionandcombine_pa_w4_kernel(tc, x1, w_words, w_scales, x2_bytes,
                 for u in range(2):
                     nc.tensor.transpose(acc[:, u, c, :], part(c, u), ident[:])
 
-        def every_second(pairs):
-            return lambda c, u: pairs[:, 256 * c + u : 256 * (c + 1) : 2]
-
         def turn_x1(i):
-            turn_pairs(("x1", i), every_second(x1_raw[i][:].bitcast(F32)))
+            pairs = x1_raw[i][:].bitcast(F32)
+            turn_pairs(("x1", i), lambda c, u: pairs[:, 256 * c + u : 256 * (c + 1) : 2])
 
         def turn_x2(i):
-            pairs = x2_wide[i][:].bitcast(F32)
-            if i == 0:
-                turn_pairs(("x2", i), lambda c, u: pairs[:, P * (2 * u + c) : P * (2 * u + c + 1)])
-            elif by_matmul(i):
+            if i in BY_MATMUL:
                 acc = take_bank(("x2", i), [P, 4, ROWS], BF16)
                 for c in range(2):
-                    for t in range(4):
-                        nc.tensor.matmul(
-                            out=acc[:, t, P * c : P * (c + 1)],
-                            lhsT=x2_wide[i][:, D * c + t : D * (c + 1) : 4],
-                            rhs=ident_bf16[:],
-                            start=True,
-                            stop=True,
-                        )
-            else:
-                turn_pairs(("x2", i), every_second(pairs))
+                    for u in range(2):
+                        first = ROWS * (2 * u + c)
+                        for e in range(2):
+                            nc.tensor.matmul(
+                                out=acc[:, 2 * u + e, P * c : P * (c + 1)],
+                                lhsT=x2_wide[i][:, first + e : first + ROWS : 2],
+                                rhs=ident_bf16[:],
+                                start=True,
+                                stop=True,
+                            )
+                return
+            pairs = x2_wide[i][:].bitcast(F32)
+            turn_pairs(("x2", i), lambda c, u: pairs[:, P * (2 * u + c) : P * (2 * u + c + 1)])
 
-        def by_matmul(i):
-            return i % 2 == 1
-
-        def empty_x1(i):
-            nc.scalar.copy(
+        def empty_x1(i, copy):
+            copy(
                 out=x1_k[i][:].bitcast(F32).rearrange("p (r u) -> p r u", u=2),
                 in_=give_bank(("x1", i))[:].rearrange("p u c r -> p (c r) u"),
             )
 
         def scale_x2(i):
             acc = give_bank(("x2", i))
-            if by_matmul(i):
+            scales = scale_col[:].rearrange("p (u e) -> p u e", u=2)[:, :, 0:2].unsqueeze(1).to_broadcast([P, ROWS, 2, 2])
+            if i in BY_MATMUL:
                 nc.vector.tensor_tensor(
-                    out=x2_k[i][:].rearrange("p (r t) -> p r t", t=4),
-                    in0=scale_col[:].unsqueeze(1).to_broadcast([P, ROWS, 4]),
-                    in1=acc[:].rearrange("p t r -> p r t"),
+                    out=x2_k[i].rearrange("p (r u e) -> p r u e", u=2, e=2),
+                    in0=scales,
+                    in1=acc[:].rearrange("p (u e) r -> p r u e", u=2),
                     op=MULT,
                 )
-            else:
-                nc.vector.tensor_tensor(
-                    out=x2_k[i][:].rearrange("p (r u e) -> p r u e", u=2, e=2),
-                    in0=scale_col[:].rearrange("p (u e) -> p u e", u=2).unsqueeze(1).to_broadcast([P, ROWS, 2, 2]),
-                    in1=acc[:].rearrange("p u c r -> p (u c r)").bitcast(BF16).rearrange("p (u r e) -> p r u e", u=2, e=2),
-                    op=MULT,
-                )
+                return
+            nc.vector.tensor_tensor(
+                out=x2_k[i].rearrange("p (r u e) -> p r u e", u=2, e=2),
+                in0=scales,
+                in1=acc[:].rearrange("p u c r -> p (u c r)").bitcast(BF16).rearrange("p (u r e) -> p r u e", u=2, e=2),
+                op=MULT,
+            )
 
         def quantize_x1(i):
             nc.vector.quantize_mx(out=x1_words[i][:].bitcast(FP8X4), scales=x1_plane[i][:], in_=x1_k[i][:])
@@ -159,56 +167,66 @@ def tile_coattentionandcombine_pa_w4_kernel(tc, x1, w_words, w_scales, x2_bytes,
         def quantize_x2(i):
             b, j = divmod(i, 2)
             cols = slice(ROWS * j, ROWS * (j + 1))
-            nc.vector.quantize_mx(out=x2_words[b][:, cols].bitcast(FP8X4), scales=x2_plane[b][:, cols], in_=x2_k[i][:])
+            nc.vector.quantize_mx(out=x2_words[b][:, cols].bitcast(FP8X4), scales=x2_plane[b][:, cols], in_=x2_k[i])
 
-        def quantize_h(i):
-            for first, count in ((0, P), (P, P)) if i == LAST else ((0, ROWS),):
-                rows = slice(first, first + count)
-                nc.vector.quantize_mx(
-                    out=h_words[i][:, rows].bitcast(FP8X4),
-                    scales=h_plane[i][:, rows],
-                    in_=h_k[i][:, 4 * first : 4 * (first + count)],
+        def quantize_x2_batch(b):
+            nc.vector.quantize_mx(out=x2_words[b][:].bitcast(FP8X4), scales=x2_plane[b][:], in_=x2_k_batch[b][:])
+
+        def quantize_h(i, first=0, count=ROWS):
+            rows = slice(first, first + count)
+            nc.vector.quantize_mx(
+                out=h_words[i][:, rows].bitcast(FP8X4),
+                scales=h_plane[i][:, rows],
+                in_=h_k[i][:, 4 * first : 4 * (first + count)],
+            )
+
+        def order_w(copy):
+            copy(
+                out=w[:].bitcast(U16).rearrange("p (u e q j) -> p u e q j", u=2, e=2, j=8),
+                in_=w_raw[:].bitcast(U16).rearrange("p (q u j e) -> p u e q j", u=2, e=2, j=8),
+            )
+
+        def order_w_plane():
+            nc.vector.tensor_copy(
+                out=w_plane[:].rearrange("p (u e q j) -> p u e q j", u=2, e=2, j=8),
+                in_=w_raw_plane[:].rearrange("p (q u j e) -> p u e q j", u=2, e=2, j=8),
+            )
+
+        def project(i, c):
+            rows = slice(P * c, P * (c + 1))
+            acc = take_bank(("h", i, c), [P, 4, P])
+            for t in range(4):
+                nc.tensor.matmul_mx(
+                    out=acc[:, t, :],
+                    lhsT=w[:, 256 * t : 256 * (t + 1)].bitcast(FP4X4),
+                    lhsT_scale=w_plane[:, P * t : P * (t + 1)],
+                    rhs=x1_words[i][:, rows].bitcast(FP8X4),
+                    rhs_scale=x1_plane[i][:, rows],
+                    start=True,
+                    stop=True,
                 )
 
-        def project(i):
-            for c in range(2):
-                rows = slice(P * c, P * (c + 1))
-                acc = take_bank(("h", i, c), [P, 4, P])
-                for t in range(4):
-                    nc.tensor.matmul_mx(
-                        out=acc[:, t, :],
-                        lhsT=w[:, 256 * t : 256 * (t + 1)].bitcast(FP4X4),
-                        lhsT_scale=w_plane[:, P * t : P * (t + 1)],
-                        rhs=x1_words[i][:, rows].bitcast(FP8X4),
-                        rhs_scale=x1_plane[i][:, rows],
-                        start=True,
-                        stop=True,
-                    )
-
-        def empty_h(i, c):
-            copy = nc.vector.tensor_copy if (c == 1 and i >= H_ON_VECTOR_FROM) or i == LAST else nc.scalar.copy
+        def empty_h(i, c, copy):
             copy(
                 out=h_k[i][:, 512 * c : 512 * (c + 1)].rearrange("p (r t) -> p r t", t=4),
                 in_=give_bank(("h", i, c))[:].rearrange("p t r -> p r t"),
             )
 
-        def compare(i):
+        def compare(i, c):
             b = i // 2
-            for c in range(2):
-                rows = slice(P * c, P * (c + 1))
-                nc.tensor.matmul_mx(
-                    out=take_bank(("sim", i, c), [P, L])[:],
-                    lhsT=h_words[i][:, rows].bitcast(FP8X4),
-                    lhsT_scale=h_plane[i][:, rows],
-                    rhs=x2_words[b][:].bitcast(FP8X4),
-                    rhs_scale=x2_plane[b][:],
-                    start=True,
-                    stop=True,
-                )
+            rows = slice(P * c, P * (c + 1))
+            nc.tensor.matmul_mx(
+                out=take_bank(("sim", i, c), [P, L])[:],
+                lhsT=h_words[i][:, rows].bitcast(FP8X4),
+                lhsT_scale=h_plane[i][:, rows],
+                rhs=x2_words[b][:].bitcast(FP8X4),
+                rhs_scale=x2_plane[b][:],
+                start=True,
+                stop=True,
+            )
 
-        def empty_sim(i, c):
+        def empty_sim(i, c, copy):
             b, j = divmod(i, 2)
-            copy = nc.vector.tensor_copy if (i, c) == (LAST, 1) else nc.scalar.copy
             rows = result[i][:, L * c : L * (c + 1)]
             copy(
                 out=rows.rearrange("p (s m e) -> p s m e", m=P, e=2),
@@ -216,61 +234,59 @@ def tile_coattentionandcombine_pa_w4_kernel(tc, x1, w_words, w_scales, x2_bytes,
             )
             nc.sync.dma_start(out=out_view[b, :, 2 * j + c, :], in_=rows)
 
-        nc.vector.memset(zeros[:], 0.0)
-        nc.vector.memset(w_raw_plane[:].bitcast(I32), 0)
-        nc.vector.memset(ones[:], 1.0)
-
-        load_x2(0)
-        nc.sync.dma_start(out=scale_col[:], in_=x2_scale.rearrange("a o (p t) -> p (a o t)", t=4))
-        load_x2(1)
-        load_x2(2)
-        nc.sync.dma_start(out=w_raw[:].bitcast(I32), in_=w_words.rearrange("g p n -> p (g n)").bitcast(I32))
-        for i in range(HALVES):
-            load_x1(i)
-            if i == 1:
-                for q in range(4):
-                    nc.sync.dma_start(
-                        out=w_raw_plane[32 * q : 32 * q + 4, :].bitcast(I32),
-                        in_=w_scales[0, 4 * q : 4 * q + 4, :].bitcast(I32),
-                    )
-            if i + 3 < HALVES:
-                load_x2(i + 3)
-
-        make_identity(nc, ident[:])
-
-        idle = take_bank("idle", [P, P])
-        for k in range(WARM_UPS):
-            nc.tensor.matmul(out=idle[:], lhsT=zeros[:], rhs=zeros[:], start=True, stop=True)
-        give_bank("idle")
+        on_vector, on_scalar, on_gpsimd = nc.vector.tensor_copy, nc.scalar.copy, nc.gpsimd.tensor_copy
 
         def at(stage, i, *more):
             if 0 <= i < HALVES:
                 stage(i, *more)
 
-        for s in range(-1 - WIDEN_AHEAD, HALVES + 5):
-            at(empty_sim, s - 5, 0)
+        def warm_up(count):
+            idle = take_bank("idle", [P, P])
+            for k in range(count):
+                nc.tensor.matmul(out=idle[:], lhsT=zeros[:], rhs=zeros[:], start=True, stop=True)
+            give_bank("idle")
 
+        nc.vector.memset(zeros[:], 0.0)
+        nc.vector.memset(w_raw_plane[:].bitcast(I32), 0)
+
+        load_x2(0)
+        load_w_plane()
+        load_scale_col()
+        load_x2(1)
+        load_x2(2)
+        load_w()
+        load_x1(0)
+        for i in range(1, HALVES):
+            if i + 2 < HALVES:
+                load_x2(i + 2)
+            load_x1(i)
+
+        make_identity(nc, ident[:])
+        warm_up(WARM_UPS)
+
+        for s in range(-3, HALVES + 5):
+            at(empty_sim, s - 5, 0, on_scalar)
             at(turn_x2, s + 1)
             at(turn_x1, s)
-
             at(scale_x2, s)
             at(quantize_x1, s - 1)
-            if s == 1:
-                nc.vector.tensor_copy(out=w_plane[:].rearrange("p (t m) -> p t m", t=4), in_=w_raw_plane[:].rearrange("p (m t) -> p t m", t=4))
-            at(empty_h, s - 3, 1)
+            at(empty_h, s - 3, 1, on_vector if s - 3 >= 2 else on_scalar)
             at(quantize_x2, s - 2)
-            at(empty_sim, s - 5, 1)
-            at(quantize_h, s - 3)
-
-            at(project, s - 2)
-            at(compare, s - 4)
-
-            at(widen, s + 1 + WIDEN_AHEAD)
-            if s == -1 - WIDEN_AHEAD:
+            at(empty_sim, s - 5, 1, on_vector if s - 5 == LAST else on_scalar)
+            if s - 3 == LAST:
+                quantize_h(LAST, 0, P)
+                quantize_h(LAST, P, P)
+            else:
+                at(quantize_h, s - 3)
+            at(project, s - 2, 0)
+            at(project, s - 2, 1)
+            at(compare, s - 4, 0)
+            at(compare, s - 4, 1)
+            at(widen, s + 3, on_vector if s == -3 else on_scalar, None)
+            if s == -3:
+                spread_w_plane()
                 nc.vector.tensor_copy(out=ident_bf16[:], in_=ident[:])
-                nc.vector.tensor_copy(
-                    out=w[:].bitcast(U16).rearrange("p (t m) -> p t m", t=4),
-                    in_=w_raw[:].bitcast(U16).rearrange("p (m t) -> p t m", t=4),
-                )
-            at(empty_x1, s)
-            at(empty_h, s - 2, 0)
+                order_w_plane()
+                order_w(on_vector)
+            at(empty_x1, s, on_scalar)
+            at(empty_h, s - 2, 0, on_vector if s - 2 == LAST else on_scalar)

@@ -53,10 +53,10 @@ def tile_coattentionandcombine_pa_w4_kernel(tc, x1, w_words, w_scales, x2_bytes,
         x2_wide = {}
         x2_k_batch = [sbuf("x2_k%d" % b, 4 * L, BF16) for b in range(B)]
         x2_k = [x2_k_batch[i // 2][:, 4 * ROWS * (i % 2) : 4 * ROWS * (i % 2 + 1)] for i in range(HALVES)]
-        scale_col = sbuf("scale_col", 16, F32)
+        scale_raw = sbuf("scale_raw", 16, F32)
+        scale_col = sbuf("scale_col", 4, F32)
         w_raw = sbuf("w_raw", 2 * D, U8)
         w_raw_plane = sbuf("w_raw_plane", D, U8)
-        w_rows = keep.tile([4, 4, D // 4], I32, name="w_rows")
         w = sbuf("w", 2 * D, U8)
         w_plane = sbuf("w_plane", D, U8)
         ident = sbuf("ident", P, F32)
@@ -76,17 +76,23 @@ def tile_coattentionandcombine_pa_w4_kernel(tc, x1, w_words, w_scales, x2_bytes,
         def load_scale_col():
             by_run = x2_scale.rearrange("a o (q u j e) -> (a o u) q j e", u=2, j=8, e=2)
             for u in range(2):
-                nc.sync.dma_start(out=scale_col[:, 8 * u : 8 * u + 2], in_=by_run[u])
+                nc.sync.dma_start(out=scale_raw[:, 8 * u : 8 * u + 2], in_=by_run[u])
+
+        def pack_scale_col():
+            nc.vector.tensor_copy(
+                out=scale_col[:].rearrange("p (u e) -> p u e", u=2),
+                in_=scale_raw[:].rearrange("p (u e) -> p u e", u=2)[:, :, 0:2],
+            )
 
         def load_w():
             nc.sync.dma_start(out=w_raw[:].bitcast(I32), in_=w_words.rearrange("g p n -> p (g n)").bitcast(I32))
 
         def load_w_plane():
-            nc.sync.dma_start(out=w_rows[:], in_=w_scales.bitcast(I32).rearrange("g (q r) n -> r (g q) n", r=4))
-
-        def spread_w_plane():
             for q in range(4):
-                nc.vector.tensor_copy(out=w_raw_plane[32 * q : 32 * q + 4, :].bitcast(I32), in_=w_rows[:, q, :])
+                nc.sync.dma_start(
+                    out=w_raw_plane[32 * q : 32 * q + 4, :].bitcast(I32),
+                    in_=w_scales[0, 4 * q : 4 * q + 4, :].bitcast(I32),
+                )
 
         free_banks = list(range(BANKS))
         held = {}
@@ -104,10 +110,13 @@ def tile_coattentionandcombine_pa_w4_kernel(tc, x1, w_words, w_scales, x2_bytes,
 
         def widen(i, copy, tag):
             x2_wide[i] = sbuf("x2_wide%d" % i, 2 * D, BF16, tag)
-            copy(
-                out=x2_wide[i][:].rearrange("p (u q k) -> p q u k", u=2, k=16),
-                in_=x2_raw[i][:].bitcast(E4M3).rearrange("p (q u k) -> p q u k", u=2, k=16),
-            )
+            if copy is on_scalar:
+                copy(out=x2_wide[i][:], in_=x2_raw[i][:].bitcast(E4M3).rearrange("p (q u k) -> p u q k", u=2, k=16))
+            else:
+                copy(
+                    out=x2_wide[i][:].rearrange("p (u q k) -> p q u k", u=2, k=16),
+                    in_=x2_raw[i][:].bitcast(E4M3).rearrange("p (q u k) -> p q u k", u=2, k=16),
+                )
 
         def turn_pairs(key, part):
             acc = take_bank(key, [P, 2, 2, P])
@@ -145,7 +154,7 @@ def tile_coattentionandcombine_pa_w4_kernel(tc, x1, w_words, w_scales, x2_bytes,
 
         def scale_x2(i):
             acc = give_bank(("x2", i))
-            scales = scale_col[:].rearrange("p (u e) -> p u e", u=2)[:, :, 0:2].unsqueeze(1).to_broadcast([P, ROWS, 2, 2])
+            scales = scale_col[:].rearrange("p (u e) -> p u e", u=2).unsqueeze(1).to_broadcast([P, ROWS, 2, 2])
             if i in BY_MATMUL:
                 nc.vector.tensor_tensor(
                     out=x2_k[i].rearrange("p (r u e) -> p r u e", u=2, e=2),
@@ -250,16 +259,16 @@ def tile_coattentionandcombine_pa_w4_kernel(tc, x1, w_words, w_scales, x2_bytes,
         nc.vector.memset(w_raw_plane[:].bitcast(I32), 0)
 
         load_x2(0)
-        load_w_plane()
         load_scale_col()
         load_x2(1)
         load_x2(2)
         load_w()
-        load_x1(0)
-        for i in range(1, HALVES):
-            if i + 2 < HALVES:
-                load_x2(i + 2)
+        for i in range(HALVES):
             load_x1(i)
+            if i == 1:
+                load_w_plane()
+            if i + 3 < HALVES:
+                load_x2(i + 3)
 
         make_identity(nc, ident[:])
         warm_up(WARM_UPS)
@@ -270,6 +279,8 @@ def tile_coattentionandcombine_pa_w4_kernel(tc, x1, w_words, w_scales, x2_bytes,
             at(turn_x1, s)
             at(scale_x2, s)
             at(quantize_x1, s - 1)
+            if s == 1:
+                order_w_plane()
             at(empty_h, s - 3, 1, on_vector if s - 3 >= 2 else on_scalar)
             at(quantize_x2, s - 2)
             at(empty_sim, s - 5, 1, on_vector if s - 5 == LAST else on_scalar)
@@ -284,9 +295,8 @@ def tile_coattentionandcombine_pa_w4_kernel(tc, x1, w_words, w_scales, x2_bytes,
             at(compare, s - 4, 1)
             at(widen, s + 3, on_vector if s == -3 else on_scalar, None)
             if s == -3:
-                spread_w_plane()
                 nc.vector.tensor_copy(out=ident_bf16[:], in_=ident[:])
-                order_w_plane()
+                pack_scale_col()
                 order_w(on_vector)
             at(empty_x1, s, on_scalar)
             at(empty_h, s - 2, 0, on_vector if s - 2 == LAST else on_scalar)

@@ -23,7 +23,7 @@ LAST = HALVES - 1
 ROWS = 256
 BANKS = 8
 WARM_UPS = 4
-BY_MATMUL = (1, 3, 5)
+BY_MATMUL = (1, 3)
 
 
 def tile_coattentionandcombine_pa_w4_kernel(tc, x1, w_words, w_scales, x2_bytes, x2_scale, out):
@@ -195,8 +195,8 @@ def tile_coattentionandcombine_pa_w4_kernel(tc, x1, w_words, w_scales, x2_bytes,
                 in_=w_raw[:].bitcast(U16).rearrange("p (q u j e) -> p u e q j", u=2, e=2, j=8),
             )
 
-        def order_w_plane():
-            nc.vector.tensor_copy(
+        def order_w_plane(copy):
+            copy(
                 out=w_plane[:].rearrange("p (u e q j) -> p u e q j", u=2, e=2, j=8),
                 in_=w_raw_plane[:].rearrange("p (q u j e) -> p u e q j", u=2, e=2, j=8),
             )
@@ -255,48 +255,122 @@ def tile_coattentionandcombine_pa_w4_kernel(tc, x1, w_words, w_scales, x2_bytes,
                 nc.tensor.matmul(out=idle[:], lhsT=zeros[:], rhs=zeros[:], start=True, stop=True)
             give_bank("idle")
 
+        TAGS = {5: "x1_k1"}
         nc.vector.memset(zeros[:], 0.0)
         nc.vector.memset(w_raw_plane[:].bitcast(I32), 0)
-
         load_x2(0)
-        load_scale_col()
         load_x2(1)
+        load_scale_col()
         load_x2(2)
+        load_x2(3)
+        load_x1(0)
         load_w()
-        for i in range(HALVES):
-            load_x1(i)
-            if i == 1:
-                load_w_plane()
-            if i + 3 < HALVES:
-                load_x2(i + 3)
+        load_x1(1)
+        load_w_plane()
+        load_x1(2)
+        load_x2(4)
+        load_x2(5)
+        load_x1(3)
+        load_x1(4)
+        load_x1(5)
 
         make_identity(nc, ident[:])
         warm_up(WARM_UPS)
-
-        for s in range(-3, HALVES + 5):
-            at(empty_sim, s - 5, 0, on_scalar)
-            at(turn_x2, s + 1)
-            at(turn_x1, s)
-            at(scale_x2, s)
-            at(quantize_x1, s - 1)
-            if s == 1:
-                order_w_plane()
-            at(empty_h, s - 3, 1, on_vector if s - 3 >= 2 else on_scalar)
-            at(quantize_x2, s - 2)
-            at(empty_sim, s - 5, 1, on_vector if s - 5 == LAST else on_scalar)
-            if s - 3 == LAST:
-                quantize_h(LAST, 0, P)
-                quantize_h(LAST, P, P)
-            else:
-                at(quantize_h, s - 3)
-            at(project, s - 2, 0)
-            at(project, s - 2, 1)
-            at(compare, s - 4, 0)
-            at(compare, s - 4, 1)
-            at(widen, s + 3, on_vector if s == -3 else on_scalar, None)
-            if s == -3:
-                nc.vector.tensor_copy(out=ident_bf16[:], in_=ident[:])
-                pack_scale_col()
-                order_w(on_vector)
-            at(empty_x1, s, on_scalar)
-            at(empty_h, s - 2, 0, on_vector if s - 2 == LAST else on_scalar)
+        widen(0, on_vector, TAGS.get(0))
+        widen(1, on_scalar, TAGS.get(1))
+        nc.vector.tensor_copy(out=ident_bf16[:], in_=ident[:])
+        pack_scale_col()
+        widen(2, on_vector, TAGS.get(2))
+        turn_x2(0)
+        widen(3, on_scalar, TAGS.get(3))
+        turn_x2(1)
+        scale_x2(0)
+        turn_x1(0)
+        order_w(on_scalar)
+        empty_x1(0, on_scalar)
+        turn_x1(1)
+        scale_x2(1)
+        order_w_plane(on_gpsimd)
+        turn_x2(2)
+        empty_x1(1, on_scalar)
+        turn_x1(2)
+        quantize_x1(0)
+        turn_x2(3)
+        quantize_x2_batch(0)
+        empty_x1(2, on_scalar)
+        quantize_x1(1)
+        project(0, 0)
+        scale_x2(2)
+        widen(5, on_gpsimd, TAGS.get(5))
+        widen(4, on_scalar, TAGS.get(4))
+        project(0, 1)
+        project(1, 0)
+        empty_h(0, 0, on_scalar)
+        project(1, 1)
+        scale_x2(3)
+        turn_x1(3)
+        empty_h(0, 1, on_scalar)
+        turn_x2(4)
+        empty_h(1, 0, on_scalar)
+        turn_x1(4)
+        quantize_x1(2)
+        quantize_h(0)
+        empty_h(1, 1, on_scalar)
+        empty_x1(3, on_vector)
+        project(2, 0)
+        empty_x1(4, on_scalar)
+        project(2, 1)
+        quantize_h(1)
+        compare(0, 0)
+        empty_h(2, 0, on_scalar)
+        quantize_x1(3)
+        compare(0, 1)
+        scale_x2(4)
+        compare(1, 0)
+        empty_sim(0, 0, on_scalar)
+        project(3, 0)
+        project(3, 1)
+        empty_sim(0, 1, on_scalar)
+        turn_x2(5)
+        quantize_x1(4)
+        empty_h(2, 1, on_scalar)
+        quantize_x2_batch(1)
+        turn_x1(5)
+        empty_h(3, 1, on_vector)
+        empty_sim(1, 0, on_scalar)
+        compare(1, 1)
+        project(4, 0)
+        quantize_h(2)
+        empty_h(3, 0, on_scalar)
+        scale_x2(5)
+        project(4, 1)
+        compare(2, 0)
+        empty_x1(5, on_scalar)
+        compare(2, 1)
+        empty_sim(1, 1, on_scalar)
+        quantize_h(3)
+        quantize_x1(5)
+        empty_h(4, 0, on_scalar)
+        empty_h(4, 1, on_vector)
+        compare(3, 0)
+        compare(3, 1)
+        empty_sim(2, 0, on_scalar)
+        quantize_x2_batch(2)
+        project(5, 0)
+        quantize_h(4)
+        project(5, 1)
+        empty_sim(2, 1, on_scalar)
+        empty_h(5, 0, on_vector)
+        compare(4, 0)
+        empty_sim(3, 0, on_scalar)
+        compare(4, 1)
+        empty_h(5, 1, on_vector)
+        empty_sim(3, 1, on_scalar)
+        quantize_h(5, 0, P)
+        quantize_h(5, 128, P)
+        empty_sim(4, 0, on_scalar)
+        compare(5, 0)
+        compare(5, 1)
+        empty_sim(4, 1, on_scalar)
+        empty_sim(5, 0, on_scalar)
+        empty_sim(5, 1, on_vector)

@@ -40,7 +40,8 @@ def tile_coattentionandcombine_pa_w4_kernel(tc, x1, w_words, w_scales, x2_bytes,
             return [sbuf("%s%d" % (name, i), width, dtype) for i in range(HALVES)]
 
         x1_raw = per_half("x1_raw", 2 * D, BF16)
-        x2_raw = per_half("x2_raw", 2 * D, U8)
+        x2_raw_last = sbuf("x2_raw_last", 4 * D, U8)
+        x2_raw = [sbuf("x2_raw%d" % i, 2 * D, U8) for i in range(HALVES - 2)] + [x2_raw_last[:, : 2 * D], x2_raw_last[:, 2 * D :]]
         x1_k = per_half("x1_k", 4 * ROWS, BF16)
         h_k = per_half("h_k", 4 * ROWS, BF16)
         x1_words = per_half("x1_words", ROWS, U32)
@@ -51,6 +52,7 @@ def tile_coattentionandcombine_pa_w4_kernel(tc, x1, w_words, w_scales, x2_bytes,
         x2_words = [sbuf("x2_words%d" % b, L, U32) for b in range(B)]
         x2_plane = [sbuf("x2_plane%d" % b, L, U8) for b in range(B)]
         x2_wide = {}
+        blocks = {}
         x2_k_batch = [sbuf("x2_k%d" % b, 4 * L, BF16) for b in range(B)]
         x2_k = [x2_k_batch[i // 2][:, 4 * ROWS * (i % 2) : 4 * ROWS * (i % 2 + 1)] for i in range(HALVES)]
         scale_raw = sbuf("scale_raw", 16, F32)
@@ -73,13 +75,16 @@ def tile_coattentionandcombine_pa_w4_kernel(tc, x1, w_words, w_scales, x2_bytes,
         def load_x2(i):
             nc.sync.dma_start(out=x2_raw[i][:], in_=x2_view[i // 2, i % 2])
 
+        def load_x2_last_batch():
+            nc.sync.dma_start(out=x2_raw_last[:].rearrange("p (j n) -> p j n", j=2), in_=x2_view[B - 1].rearrange("j p n -> p j n"))
+
         def load_scale_col():
             by_run = x2_scale.rearrange("a o (q u j e) -> (a o u) q j e", u=2, j=8, e=2)
             for u in range(2):
                 nc.sync.dma_start(out=scale_raw[:, 8 * u : 8 * u + 2], in_=by_run[u])
 
-        def pack_scale_col():
-            nc.vector.tensor_copy(
+        def pack_scale_col(copy):
+            copy(
                 out=scale_col[:].rearrange("p (u e) -> p u e", u=2),
                 in_=scale_raw[:].rearrange("p (u e) -> p u e", u=2)[:, :, 0:2],
             )
@@ -110,13 +115,33 @@ def tile_coattentionandcombine_pa_w4_kernel(tc, x1, w_words, w_scales, x2_bytes,
 
         def widen(i, copy, tag):
             x2_wide[i] = sbuf("x2_wide%d" % i, 2 * D, BF16, tag)
+            blocks[i, 0], blocks[i, 1] = x2_wide[i][:, :D], x2_wide[i][:, D:]
             if copy is on_scalar:
-                copy(out=x2_wide[i][:], in_=x2_raw[i][:].bitcast(E4M3).rearrange("p (q u k) -> p u q k", u=2, k=16))
+                copy(out=x2_wide[i][:], in_=x2_raw[i][:].bitcast(E4M3).rearrange("p (c q u k) -> p c u q k", c=2, u=2, k=16))
             else:
                 copy(
-                    out=x2_wide[i][:].rearrange("p (u q k) -> p q u k", u=2, k=16),
-                    in_=x2_raw[i][:].bitcast(E4M3).rearrange("p (q u k) -> p q u k", u=2, k=16),
+                    out=x2_wide[i][:].rearrange("p (c u q k) -> p c q u k", c=2, u=2, k=16),
+                    in_=x2_raw[i][:].bitcast(E4M3).rearrange("p (c q u k) -> p c q u k", c=2, u=2, k=16),
                 )
+
+        def widen_block(i, c, copy, tag=None):
+            if i not in x2_wide:
+                x2_wide[i] = sbuf("x2_wide%d" % i, 2 * D, BF16, tag)
+            wide = x2_wide[i][:, D * c : D * (c + 1)]
+            blocks[i, c] = wide
+            codes = x2_raw[i][:, D * c : D * (c + 1)].bitcast(E4M3).rearrange("p (q u k) -> p u q k", u=2, k=16)
+            if copy is on_scalar:
+                copy(out=wide, in_=codes)
+            else:
+                copy(out=wide.rearrange("p (u q k) -> p q u k", u=2, k=16), in_=codes.rearrange("p u q k -> p q u k"))
+
+        def widen_last_on_gpsimd(tag):
+            rest = sbuf("x2_wide_rest", 3 * D, BF16, tag)
+            blocks[4, 1], blocks[5, 0], blocks[5, 1] = rest[:, :D], rest[:, D : 2 * D], rest[:, 2 * D :]
+            nc.gpsimd.tensor_copy(
+                out=rest[:].rearrange("p (c u q k) -> p c q u k", c=3, u=2, k=16),
+                in_=x2_raw_last[:, D:].bitcast(E4M3).rearrange("p (c q u k) -> p c q u k", c=3, u=2, k=16),
+            )
 
         def turn_pairs(key, part):
             acc = take_bank(key, [P, 2, 2, P])
@@ -133,7 +158,7 @@ def tile_coattentionandcombine_pa_w4_kernel(tc, x1, w_words, w_scales, x2_bytes,
                 acc = take_bank(("x2", i), [P, 4, ROWS], BF16)
                 for c in range(2):
                     for u in range(2):
-                        first = ROWS * (2 * u + c)
+                        first = ROWS * (2 * c + u)
                         for e in range(2):
                             nc.tensor.matmul(
                                 out=acc[:, 2 * u + e, P * c : P * (c + 1)],
@@ -143,8 +168,7 @@ def tile_coattentionandcombine_pa_w4_kernel(tc, x1, w_words, w_scales, x2_bytes,
                                 stop=True,
                             )
                 return
-            pairs = x2_wide[i][:].bitcast(F32)
-            turn_pairs(("x2", i), lambda c, u: pairs[:, P * (2 * u + c) : P * (2 * u + c + 1)])
+            turn_pairs(("x2", i), lambda c, u: blocks[i, c].bitcast(F32)[:, P * u : P * (u + 1)])
 
         def empty_x1(i, copy):
             copy(
@@ -255,7 +279,7 @@ def tile_coattentionandcombine_pa_w4_kernel(tc, x1, w_words, w_scales, x2_bytes,
                 nc.tensor.matmul(out=idle[:], lhsT=zeros[:], rhs=zeros[:], start=True, stop=True)
             give_bank("idle")
 
-        TAGS = {5: "x1_k1"}
+        TAGS = {4: "x1_k1"}
         nc.vector.memset(zeros[:], 0.0)
         nc.vector.memset(w_raw_plane[:].bitcast(I32), 0)
         load_x2(0)
@@ -264,113 +288,113 @@ def tile_coattentionandcombine_pa_w4_kernel(tc, x1, w_words, w_scales, x2_bytes,
         load_x2(2)
         load_x2(3)
         load_x1(0)
-        load_w()
         load_x1(1)
         load_w_plane()
         load_x1(2)
-        load_x2(4)
-        load_x2(5)
+        load_w()
         load_x1(3)
+        load_x2_last_batch()
         load_x1(4)
         load_x1(5)
 
         make_identity(nc, ident[:])
         warm_up(WARM_UPS)
-        widen(0, on_vector, TAGS.get(0))
-        widen(1, on_scalar, TAGS.get(1))
-        nc.vector.tensor_copy(out=ident_bf16[:], in_=ident[:])
-        pack_scale_col()
-        widen(2, on_vector, TAGS.get(2))
+        widen_block(0, 0, on_vector)
+        widen_block(0, 1, on_scalar)
+        widen(1, on_vector, TAGS.get(1))
+        on_scalar(out=ident_bf16[:], in_=ident[:])
+        pack_scale_col(on_scalar)
+        widen(2, on_scalar, TAGS.get(2))
         turn_x2(0)
         widen(3, on_scalar, TAGS.get(3))
         turn_x2(1)
         scale_x2(0)
         turn_x1(0)
-        order_w(on_scalar)
-        empty_x1(0, on_scalar)
         turn_x1(1)
         scale_x2(1)
+        empty_x1(0, on_scalar)
         order_w_plane(on_gpsimd)
         turn_x2(2)
         empty_x1(1, on_scalar)
         turn_x1(2)
         quantize_x1(0)
         turn_x2(3)
+        order_w(on_scalar)
         quantize_x2_batch(0)
         empty_x1(2, on_scalar)
         quantize_x1(1)
-        project(0, 0)
+        turn_x1(3)
         scale_x2(2)
-        widen(5, on_gpsimd, TAGS.get(5))
-        widen(4, on_scalar, TAGS.get(4))
+        project(0, 0)
+        widen_block(4, 0, on_scalar)
+        widen_last_on_gpsimd(TAGS[4])
         project(0, 1)
         project(1, 0)
-        empty_h(0, 0, on_scalar)
-        project(1, 1)
+        empty_x1(3, on_scalar)
         scale_x2(3)
-        turn_x1(3)
-        empty_h(0, 1, on_scalar)
-        turn_x2(4)
-        empty_h(1, 0, on_scalar)
+        project(1, 1)
+        empty_h(0, 0, on_scalar)
         turn_x1(4)
-        quantize_x1(2)
-        quantize_h(0)
-        empty_h(1, 1, on_scalar)
-        empty_x1(3, on_vector)
-        project(2, 0)
-        empty_x1(4, on_scalar)
-        project(2, 1)
-        quantize_h(1)
-        compare(0, 0)
-        empty_h(2, 0, on_scalar)
-        quantize_x1(3)
-        compare(0, 1)
-        scale_x2(4)
-        compare(1, 0)
-        empty_sim(0, 0, on_scalar)
-        project(3, 0)
-        project(3, 1)
-        empty_sim(0, 1, on_scalar)
-        turn_x2(5)
-        quantize_x1(4)
-        empty_h(2, 1, on_scalar)
-        quantize_x2_batch(1)
+        empty_h(0, 1, on_scalar)
         turn_x1(5)
-        empty_h(3, 1, on_vector)
+        quantize_x1(2)
+        quantize_x2_batch(1)
+        empty_h(1, 0, on_scalar)
+        quantize_x1(3)
+        project(2, 0)
+        quantize_h(0)
+        project(2, 1)
+        empty_x1(4, on_scalar)
+        empty_h(1, 1, on_vector)
+        turn_x2(4)
+        empty_x1(5, on_scalar)
+        compare(0, 0)
+        quantize_x1(4)
+        compare(0, 1)
+        empty_h(2, 0, on_scalar)
+        project(3, 0)
+        quantize_h(1)
+        scale_x2(4)
+        project(3, 1)
+        empty_h(2, 1, on_scalar)
+        compare(1, 0)
+        turn_x2(5)
+        empty_sim(0, 0, on_scalar)
+        quantize_h(2)
+        empty_h(3, 1, on_scalar)
+        quantize_x1(5)
+        project(4, 0)
+        empty_h(3, 0, on_vector)
+        compare(2, 0)
+        empty_sim(0, 1, on_scalar)
+        project(4, 1)
+        scale_x2(5)
+        compare(2, 1)
         empty_sim(1, 0, on_scalar)
         compare(1, 1)
-        project(4, 0)
-        quantize_h(2)
-        empty_h(3, 0, on_scalar)
-        scale_x2(5)
-        project(4, 1)
-        compare(2, 0)
-        empty_x1(5, on_scalar)
-        compare(2, 1)
-        empty_sim(1, 1, on_scalar)
-        quantize_h(3)
-        quantize_x1(5)
-        empty_h(4, 0, on_scalar)
-        empty_h(4, 1, on_vector)
-        compare(3, 0)
-        compare(3, 1)
-        empty_sim(2, 0, on_scalar)
-        quantize_x2_batch(2)
         project(5, 0)
-        quantize_h(4)
+        empty_sim(2, 0, on_scalar)
+        quantize_h(3)
+        empty_h(4, 0, on_scalar)
+        empty_sim(1, 1, on_vector)
         project(5, 1)
+        compare(3, 0)
+        empty_h(4, 1, on_scalar)
+        quantize_x2_batch(2)
+        compare(3, 1)
         empty_sim(2, 1, on_scalar)
+        quantize_h(4)
+        empty_sim(3, 0, on_scalar)
         empty_h(5, 0, on_vector)
         compare(4, 0)
-        empty_sim(3, 0, on_scalar)
-        compare(4, 1)
-        empty_h(5, 1, on_vector)
         empty_sim(3, 1, on_scalar)
+        empty_h(5, 1, on_vector)
+        compare(4, 1)
+        empty_sim(4, 0, on_scalar)
         quantize_h(5, 0, P)
         quantize_h(5, 128, P)
-        empty_sim(4, 0, on_scalar)
+        empty_sim(4, 1, on_vector)
         compare(5, 0)
         compare(5, 1)
-        empty_sim(4, 1, on_scalar)
         empty_sim(5, 0, on_scalar)
         empty_sim(5, 1, on_vector)

@@ -267,6 +267,28 @@ def tile_coattentionandcombine_pa_w4_kernel(tc, x1, w_words, w_scales, x2_bytes,
             )
             nc.sync.dma_start(out=out_view[b, :, 2 * j + c, :], in_=rows)
 
+        def compare_part(i, c, j):
+            b = i // 2
+            rows = slice(P * c, P * (c + 1))
+            cols = slice(ROWS * j, ROWS * (j + 1))
+            nc.tensor.matmul_mx(
+                out=take_bank(("sim", i, c, j), [P, ROWS])[:],
+                lhsT=h_words[i][:, rows].bitcast(FP8X4),
+                lhsT_scale=h_plane[i][:, rows],
+                rhs=x2_words[b][:, cols].bitcast(FP8X4),
+                rhs_scale=x2_plane[b][:, cols],
+                start=True,
+                stop=True,
+            )
+
+        def empty_sim_part(i, c, j, copy):
+            part = result[i][:, L * c + ROWS * j : L * c + ROWS * (j + 1)]
+            copy(
+                out=part.rearrange("p (m e) -> p m e", e=2),
+                in_=give_bank(("sim", i, c, j))[:].rearrange("p (e m) -> p m e", e=2),
+            )
+            nc.sync.dma_start(out=out_view[i // 2, :, 2 * (i % 2) + c, ROWS * j : ROWS * (j + 1)], in_=part)
+
         on_vector, on_scalar, on_gpsimd = nc.vector.tensor_copy, nc.scalar.copy, nc.gpsimd.tensor_copy
 
         def at(stage, i, *more):
@@ -320,81 +342,85 @@ def tile_coattentionandcombine_pa_w4_kernel(tc, x1, w_words, w_scales, x2_bytes,
         quantize_x1(0)
         turn_x2(3)
         order_w(on_scalar)
-        quantize_x2_batch(0)
+        quantize_x2(0)
         empty_x1(2, on_scalar)
         quantize_x1(1)
         turn_x1(3)
-        scale_x2(2)
+        quantize_x2(1)
         project(0, 0)
+        scale_x2(2)
         widen_block(4, 0, on_scalar)
         widen_last_on_gpsimd(TAGS[4])
         project(0, 1)
         project(1, 0)
         empty_x1(3, on_scalar)
-        scale_x2(3)
         project(1, 1)
+        scale_x2(3)
         empty_h(0, 0, on_scalar)
         turn_x1(4)
         empty_h(0, 1, on_scalar)
         turn_x1(5)
         quantize_x1(2)
-        quantize_x2_batch(1)
         empty_h(1, 0, on_scalar)
+        quantize_x2_batch(1)
         quantize_x1(3)
         project(2, 0)
+        empty_x1(4, on_scalar)
         quantize_h(0)
         project(2, 1)
-        empty_x1(4, on_scalar)
         empty_h(1, 1, on_vector)
-        turn_x2(4)
         empty_x1(5, on_scalar)
+        turn_x2(4)
         compare(0, 0)
         quantize_x1(4)
-        compare(0, 1)
         empty_h(2, 0, on_scalar)
-        project(3, 0)
+        compare(0, 1)
         quantize_h(1)
+        project(3, 0)
         scale_x2(4)
-        project(3, 1)
         empty_h(2, 1, on_scalar)
+        project(3, 1)
         compare(1, 0)
-        turn_x2(5)
         empty_sim(0, 0, on_scalar)
+        turn_x2(5)
         quantize_h(2)
-        empty_h(3, 1, on_scalar)
+        empty_sim(0, 1, on_scalar)
         quantize_x1(5)
+        compare(1, 1)
         project(4, 0)
         empty_h(3, 0, on_vector)
+        empty_h(3, 1, on_scalar)
         compare(2, 0)
-        empty_sim(0, 1, on_scalar)
-        project(4, 1)
         scale_x2(5)
-        compare(2, 1)
         empty_sim(1, 0, on_scalar)
-        compare(1, 1)
+        project(4, 1)
+        compare(2, 1)
+        empty_sim(1, 1, on_scalar)
         project(5, 0)
-        empty_sim(2, 0, on_scalar)
         quantize_h(3)
         empty_h(4, 0, on_scalar)
-        empty_sim(1, 1, on_vector)
-        project(5, 1)
-        compare(3, 0)
-        empty_h(4, 1, on_scalar)
         quantize_x2_batch(2)
+        project(5, 1)
+        empty_h(4, 1, on_vector)
+        empty_sim(2, 0, on_scalar)
+        compare(3, 0)
         compare(3, 1)
+        quantize_h(4, 0, P)
         empty_sim(2, 1, on_scalar)
-        quantize_h(4)
-        empty_sim(3, 0, on_scalar)
         empty_h(5, 0, on_vector)
+        empty_sim(3, 0, on_scalar)
         compare(4, 0)
+        quantize_h(4, 128, P)
         empty_sim(3, 1, on_scalar)
+        quantize_h(5, 0, P)
         empty_h(5, 1, on_vector)
         compare(4, 1)
         empty_sim(4, 0, on_scalar)
-        quantize_h(5, 0, P)
-        quantize_h(5, 128, P)
-        empty_sim(4, 1, on_vector)
         compare(5, 0)
-        compare(5, 1)
+        empty_sim(4, 1, on_scalar)
+        quantize_h(5, 128, P)
         empty_sim(5, 0, on_scalar)
-        empty_sim(5, 1, on_vector)
+        compare_part(5, 1, 0)
+        compare_part(5, 1, 1)
+        empty_sim_part(5, 1, 0, on_vector)
+        empty_sim_part(5, 1, 1, on_scalar)

from contextlib import ExitStack

import concourse.mybir as mybir
from concourse.masks import make_identity

B, L, D = 3, 512, 512
P = 128
FLOPS = 2 * 2 * B * L * L * D

F32 = mybir.dt.float32
BF16 = mybir.dt.bfloat16
I32 = mybir.dt.int32
U32 = mybir.dt.uint32
U8 = mybir.dt.uint8
U16 = mybir.dt.uint16
E4M3 = mybir.dt.float8_e4m3fn
FP8X4 = mybir.dt.float8_e4m3fn_x4
FP4X4 = mybir.dt.float4_e2m1fn_x4
MULT = mybir.AluOpType.mult

HALVES = 2 * B
LAST = HALVES - 1
ROWS = 256
BANKS = 8
WARM_UPS = 4
BY_MATMUL = (1, 3)


def tile_coattentionandcombine_pa_w4_kernel(tc, x1, w_words, w_scales, x2_bytes, x2_scale, out):
    nc = tc.nc
    with ExitStack() as ctx:
        keep = ctx.enter_context(tc.tile_pool(name="keep", bufs=1))
        psum = ctx.enter_context(tc.psum_pool(name="psum", bufs=1))
        ctx.enter_context(tc.manual_schedule())

        def sbuf(name, width, dtype, tag=None):
            return keep.tile([P, width], dtype, name=name, tag=tag or name, align_bytes=64)

        def per_half(name, width, dtype):
            return [sbuf("%s%d" % (name, i), width, dtype) for i in range(HALVES)]

        x1_raw = per_half("x1_raw", 2 * D, BF16)
        x2_raw_last = sbuf("x2_raw_last", 4 * D, U8)
        x2_raw = [sbuf("x2_raw%d" % i, 2 * D, U8) for i in range(HALVES - 2)] + [x2_raw_last[:, : 2 * D], x2_raw_last[:, 2 * D :]]
        x1_k = per_half("x1_k", 4 * ROWS, BF16)
        h_k = per_half("h_k", 4 * ROWS, BF16)
        x1_words = per_half("x1_words", ROWS, U32)
        x1_plane = per_half("x1_plane", ROWS, U8)
        h_words = per_half("h_words", ROWS, U32)
        h_plane = per_half("h_plane", ROWS, U8)
        result = per_half("result", 2 * L, F32)
        x2_words = [sbuf("x2_words%d" % b, L, U32) for b in range(B)]
        x2_plane = [sbuf("x2_plane%d" % b, L, U8) for b in range(B)]
        x2_wide = {}
        blocks = {}
        x2_k_batch = [sbuf("x2_k%d" % b, 4 * L, BF16) for b in range(B)]
        x2_k = [x2_k_batch[i // 2][:, 4 * ROWS * (i % 2) : 4 * ROWS * (i % 2 + 1)] for i in range(HALVES)]
        scale_raw = sbuf("scale_raw", 16, F32)
        scale_col = sbuf("scale_col", 4, F32)
        w_raw = sbuf("w_raw", 2 * D, U8)
        w_raw_plane = sbuf("w_raw_plane", D, U8)
        w = sbuf("w", 2 * D, U8)
        w_plane = sbuf("w_plane", D, U8)
        ident = sbuf("ident", P, F32)
        ident_bf16 = sbuf("ident_bf16", P, BF16)
        zeros = sbuf("zeros", P, F32)

        x1_view = x1.rearrange("b (p j c) k -> b j p (c k)", j=2, c=2)
        x2_view = x2_bytes.rearrange("b (j p c) k -> b j p (c k)", j=2, c=2)
        out_view = out.rearrange("b (p c) n -> b p c n", c=4)

        def load_x1(i):
            nc.sync.dma_start(out=x1_raw[i][:], in_=x1_view[i // 2, i % 2])

        def load_x2(i):
            nc.sync.dma_start(out=x2_raw[i][:], in_=x2_view[i // 2, i % 2])

        def load_x2_last_batch():
            nc.sync.dma_start(out=x2_raw_last[:].rearrange("p (j n) -> p j n", j=2), in_=x2_view[B - 1].rearrange("j p n -> p j n"))

        def load_scale_col():
            by_run = x2_scale.rearrange("a o (q u j e) -> (a o u) q j e", u=2, j=8, e=2)
            for u in range(2):
                nc.sync.dma_start(out=scale_raw[:, 8 * u : 8 * u + 2], in_=by_run[u])

        def pack_scale_col(copy):
            copy(
                out=scale_col[:].rearrange("p (u e) -> p u e", u=2),
                in_=scale_raw[:].rearrange("p (u e) -> p u e", u=2)[:, :, 0:2],
            )

        def load_w():
            nc.sync.dma_start(out=w_raw[:].bitcast(I32), in_=w_words.rearrange("g p n -> p (g n)").bitcast(I32))

        def load_w_plane():
            for q in range(4):
                nc.sync.dma_start(
                    out=w_raw_plane[32 * q : 32 * q + 4, :].bitcast(I32),
                    in_=w_scales[0, 4 * q : 4 * q + 4, :].bitcast(I32),
                )

        free_banks = list(range(BANKS))
        held = {}

        def take_bank(key, shape, dtype=F32):
            bank = free_banks.pop(0)
            acc = psum.tile(shape, dtype, name="bank%d" % bank, tag="bank%d" % bank)
            held[key] = bank, acc
            return acc

        def give_bank(key):
            bank, acc = held.pop(key)
            free_banks.append(bank)
            return acc

        def widen(i, copy, tag):
            x2_wide[i] = sbuf("x2_wide%d" % i, 2 * D, BF16, tag)
            blocks[i, 0], blocks[i, 1] = x2_wide[i][:, :D], x2_wide[i][:, D:]
            if copy is on_scalar:
                copy(out=x2_wide[i][:], in_=x2_raw[i][:].bitcast(E4M3).rearrange("p (c q u k) -> p c u q k", c=2, u=2, k=16))
            else:
                copy(
                    out=x2_wide[i][:].rearrange("p (c u q k) -> p c q u k", c=2, u=2, k=16),
                    in_=x2_raw[i][:].bitcast(E4M3).rearrange("p (c q u k) -> p c q u k", c=2, u=2, k=16),
                )

        def widen_block(i, c, copy, tag=None):
            if i not in x2_wide:
                x2_wide[i] = sbuf("x2_wide%d" % i, 2 * D, BF16, tag)
            wide = x2_wide[i][:, D * c : D * (c + 1)]
            blocks[i, c] = wide
            codes = x2_raw[i][:, D * c : D * (c + 1)].bitcast(E4M3).rearrange("p (q u k) -> p u q k", u=2, k=16)
            if copy is on_scalar:
                copy(out=wide, in_=codes)
            else:
                copy(out=wide.rearrange("p (u q k) -> p q u k", u=2, k=16), in_=codes.rearrange("p u q k -> p q u k"))

        def widen_last_on_gpsimd(tag):
            rest = sbuf("x2_wide_rest", 3 * D, BF16, tag)
            blocks[4, 1], blocks[5, 0], blocks[5, 1] = rest[:, :D], rest[:, D : 2 * D], rest[:, 2 * D :]
            nc.gpsimd.tensor_copy(
                out=rest[:].rearrange("p (c u q k) -> p c q u k", c=3, u=2, k=16),
                in_=x2_raw_last[:, D:].bitcast(E4M3).rearrange("p (c q u k) -> p c q u k", c=3, u=2, k=16),
            )

        def turn_pairs(key, part):
            acc = take_bank(key, [P, 2, 2, P])
            for c in range(2):
                for u in range(2):
                    nc.tensor.transpose(acc[:, u, c, :], part(c, u), ident[:])

        def turn_x1(i):
            pairs = x1_raw[i][:].bitcast(F32)
            turn_pairs(("x1", i), lambda c, u: pairs[:, 256 * c + u : 256 * (c + 1) : 2])

        def turn_x2(i):
            if i in BY_MATMUL:
                acc = take_bank(("x2", i), [P, 4, ROWS], BF16)
                for c in range(2):
                    for u in range(2):
                        first = ROWS * (2 * c + u)
                        for e in range(2):
                            nc.tensor.matmul(
                                out=acc[:, 2 * u + e, P * c : P * (c + 1)],
                                lhsT=x2_wide[i][:, first + e : first + ROWS : 2],
                                rhs=ident_bf16[:],
                                start=True,
                                stop=True,
                            )
                return
            turn_pairs(("x2", i), lambda c, u: blocks[i, c].bitcast(F32)[:, P * u : P * (u + 1)])

        def empty_x1(i, copy):
            copy(
                out=x1_k[i][:].bitcast(F32).rearrange("p (r u) -> p r u", u=2),
                in_=give_bank(("x1", i))[:].rearrange("p u c r -> p (c r) u"),
            )

        def scale_x2(i):
            acc = give_bank(("x2", i))
            scales = scale_col[:].rearrange("p (u e) -> p u e", u=2).unsqueeze(1).to_broadcast([P, ROWS, 2, 2])
            if i in BY_MATMUL:
                nc.vector.tensor_tensor(
                    out=x2_k[i].rearrange("p (r u e) -> p r u e", u=2, e=2),
                    in0=scales,
                    in1=acc[:].rearrange("p (u e) r -> p r u e", u=2),
                    op=MULT,
                )
                return
            nc.vector.tensor_tensor(
                out=x2_k[i].rearrange("p (r u e) -> p r u e", u=2, e=2),
                in0=scales,
                in1=acc[:].rearrange("p u c r -> p (u c r)").bitcast(BF16).rearrange("p (u r e) -> p r u e", u=2, e=2),
                op=MULT,
            )

        def quantize_x1(i):
            nc.vector.quantize_mx(out=x1_words[i][:].bitcast(FP8X4), scales=x1_plane[i][:], in_=x1_k[i][:])

        def quantize_x2(i):
            b, j = divmod(i, 2)
            cols = slice(ROWS * j, ROWS * (j + 1))
            nc.vector.quantize_mx(out=x2_words[b][:, cols].bitcast(FP8X4), scales=x2_plane[b][:, cols], in_=x2_k[i])

        def quantize_x2_batch(b):
            nc.vector.quantize_mx(out=x2_words[b][:].bitcast(FP8X4), scales=x2_plane[b][:], in_=x2_k_batch[b][:])

        def quantize_h(i, first=0, count=ROWS):
            rows = slice(first, first + count)
            nc.vector.quantize_mx(
                out=h_words[i][:, rows].bitcast(FP8X4),
                scales=h_plane[i][:, rows],
                in_=h_k[i][:, 4 * first : 4 * (first + count)],
            )

        def order_w(copy):
            copy(
                out=w[:].bitcast(U16).rearrange("p (u e q j) -> p u e q j", u=2, e=2, j=8),
                in_=w_raw[:].bitcast(U16).rearrange("p (q u j e) -> p u e q j", u=2, e=2, j=8),
            )

        def order_w_plane(copy):
            copy(
                out=w_plane[:].rearrange("p (u e q j) -> p u e q j", u=2, e=2, j=8),
                in_=w_raw_plane[:].rearrange("p (q u j e) -> p u e q j", u=2, e=2, j=8),
            )

        def project(i, c):
            rows = slice(P * c, P * (c + 1))
            acc = take_bank(("h", i, c), [P, 4, P])
            for t in range(4):
                nc.tensor.matmul_mx(
                    out=acc[:, t, :],
                    lhsT=w[:, 256 * t : 256 * (t + 1)].bitcast(FP4X4),
                    lhsT_scale=w_plane[:, P * t : P * (t + 1)],
                    rhs=x1_words[i][:, rows].bitcast(FP8X4),
                    rhs_scale=x1_plane[i][:, rows],
                    start=True,
                    stop=True,
                )

        def empty_h(i, c, copy):
            copy(
                out=h_k[i][:, 512 * c : 512 * (c + 1)].rearrange("p (r t) -> p r t", t=4),
                in_=give_bank(("h", i, c))[:].rearrange("p t r -> p r t"),
            )

        def compare(i, c):
            b = i // 2
            rows = slice(P * c, P * (c + 1))
            nc.tensor.matmul_mx(
                out=take_bank(("sim", i, c), [P, L])[:],
                lhsT=h_words[i][:, rows].bitcast(FP8X4),
                lhsT_scale=h_plane[i][:, rows],
                rhs=x2_words[b][:].bitcast(FP8X4),
                rhs_scale=x2_plane[b][:],
                start=True,
                stop=True,
            )

        def empty_sim(i, c, copy):
            b, j = divmod(i, 2)
            rows = result[i][:, L * c : L * (c + 1)]
            copy(
                out=rows.rearrange("p (s m e) -> p s m e", m=P, e=2),
                in_=give_bank(("sim", i, c))[:].rearrange("p (s e m) -> p s m e", m=P, e=2),
            )
            nc.sync.dma_start(out=out_view[b, :, 2 * j + c, :], in_=rows)

        def compare_part(i, c, j):
            b = i // 2
            rows = slice(P * c, P * (c + 1))
            cols = slice(ROWS * j, ROWS * (j + 1))
            nc.tensor.matmul_mx(
                out=take_bank(("sim", i, c, j), [P, ROWS])[:],
                lhsT=h_words[i][:, rows].bitcast(FP8X4),
                lhsT_scale=h_plane[i][:, rows],
                rhs=x2_words[b][:, cols].bitcast(FP8X4),
                rhs_scale=x2_plane[b][:, cols],
                start=True,
                stop=True,
            )

        def empty_sim_part(i, c, j, copy):
            part = result[i][:, L * c + ROWS * j : L * c + ROWS * (j + 1)]
            copy(
                out=part.rearrange("p (m e) -> p m e", e=2),
                in_=give_bank(("sim", i, c, j))[:].rearrange("p (e m) -> p m e", e=2),
            )
            nc.sync.dma_start(out=out_view[i // 2, :, 2 * (i % 2) + c, ROWS * j : ROWS * (j + 1)], in_=part)

        on_vector, on_scalar, on_gpsimd = nc.vector.tensor_copy, nc.scalar.copy, nc.gpsimd.tensor_copy

        def at(stage, i, *more):
            if 0 <= i < HALVES:
                stage(i, *more)

        def warm_up(count):
            idle = take_bank("idle", [P, P])
            for k in range(count):
                nc.tensor.matmul(out=idle[:], lhsT=zeros[:], rhs=zeros[:], start=True, stop=True)
            give_bank("idle")

        TAGS = {4: "x1_k1"}
        nc.vector.memset(zeros[:], 0.0)
        nc.vector.memset(w_raw_plane[:].bitcast(I32), 0)
        load_x2(0)
        load_x2(1)
        load_scale_col()
        load_x2(2)
        load_x2(3)
        load_x1(0)
        load_x1(1)
        load_w_plane()
        load_x1(2)
        load_w()
        load_x1(3)
        load_x2_last_batch()
        load_x1(4)
        load_x1(5)

        make_identity(nc, ident[:])
        warm_up(WARM_UPS)
        widen_block(0, 0, on_vector)
        widen_block(0, 1, on_scalar)
        widen(1, on_vector, TAGS.get(1))
        on_scalar(out=ident_bf16[:], in_=ident[:])
        pack_scale_col(on_scalar)
        widen(2, on_scalar, TAGS.get(2))
        turn_x2(0)
        widen(3, on_scalar, TAGS.get(3))
        turn_x2(1)
        scale_x2(0)
        turn_x1(0)
        turn_x1(1)
        scale_x2(1)
        empty_x1(0, on_scalar)
        order_w_plane(on_gpsimd)
        turn_x2(2)
        empty_x1(1, on_scalar)
        turn_x1(2)
        quantize_x1(0)
        turn_x2(3)
        order_w(on_scalar)
        quantize_x2(0)
        empty_x1(2, on_scalar)
        quantize_x1(1)
        turn_x1(3)
        quantize_x2(1)
        project(0, 0)
        scale_x2(2)
        widen_block(4, 0, on_scalar)
        widen_last_on_gpsimd(TAGS[4])
        project(0, 1)
        project(1, 0)
        empty_x1(3, on_scalar)
        project(1, 1)
        scale_x2(3)
        empty_h(0, 0, on_scalar)
        turn_x1(4)
        empty_h(0, 1, on_scalar)
        turn_x1(5)
        quantize_x1(2)
        empty_h(1, 0, on_scalar)
        quantize_x2_batch(1)
        quantize_x1(3)
        project(2, 0)
        empty_x1(4, on_scalar)
        quantize_h(0)
        project(2, 1)
        empty_h(1, 1, on_vector)
        empty_x1(5, on_scalar)
        turn_x2(4)
        compare(0, 0)
        quantize_x1(4)
        empty_h(2, 0, on_scalar)
        compare(0, 1)
        quantize_h(1)
        project(3, 0)
        scale_x2(4)
        empty_h(2, 1, on_scalar)
        project(3, 1)
        compare(1, 0)
        empty_sim(0, 0, on_scalar)
        turn_x2(5)
        quantize_h(2)
        empty_sim(0, 1, on_scalar)
        quantize_x1(5)
        compare(1, 1)
        project(4, 0)
        empty_h(3, 0, on_vector)
        empty_h(3, 1, on_scalar)
        compare(2, 0)
        scale_x2(5)
        empty_sim(1, 0, on_scalar)
        project(4, 1)
        compare(2, 1)
        empty_sim(1, 1, on_scalar)
        project(5, 0)
        quantize_h(3)
        empty_h(4, 0, on_scalar)
        quantize_x2_batch(2)
        project(5, 1)
        empty_h(4, 1, on_vector)
        empty_sim(2, 0, on_scalar)
        compare(3, 0)
        compare(3, 1)
        quantize_h(4, 0, P)
        empty_sim(2, 1, on_scalar)
        empty_h(5, 0, on_vector)
        empty_sim(3, 0, on_scalar)
        compare(4, 0)
        quantize_h(4, 128, P)
        empty_sim(3, 1, on_scalar)
        quantize_h(5, 0, P)
        empty_h(5, 1, on_vector)
        compare(4, 1)
        empty_sim(4, 0, on_scalar)
        compare(5, 0)
        empty_sim(4, 1, on_scalar)
        quantize_h(5, 128, P)
        empty_sim(5, 0, on_scalar)
        compare_part(5, 1, 0)
        compare_part(5, 1, 1)
        empty_sim_part(5, 1, 0, on_vector)
        empty_sim_part(5, 1, 1, on_scalar)
